import numpy as np
import ml_dtypes


def mxq(x, axis, fmt="e4m3"):
    dtype, down = {"e4m3": (ml_dtypes.float8_e4m3fn, 7), "e5m2": (ml_dtypes.float8_e5m2, 14)}[fmt]
    v = np.moveaxis(np.asarray(x, np.float32).astype(ml_dtypes.bfloat16).astype(np.float64), axis, -1)
    blocks = v.reshape(v.shape[:-1] + (-1, 32))
    amax = np.abs(blocks).max(-1, keepdims=True)
    byte = np.maximum(np.where(amax > 0, np.frexp(amax)[1] - 1 + 127, 0) - down, 1)
    scale = np.exp2(byte - 127.0)
    codes = (blocks / scale).astype(np.float32).astype(dtype).astype(np.float64)
    return np.moveaxis((codes * scale).reshape(v.shape), -1, axis)


WIDE = False


def mx_kscale(k):
    if not WIDE:
        return np.ones(k)
    levels = np.array([10, -10, 5, -5, 0])
    if k % 512:
        return np.exp2(np.random.permutation(np.resize(levels, k // 32))).repeat(32)
    a = np.empty((k // 512, 16))
    for p in range(k // 512):
        a[p, :8] = np.random.permutation(np.resize(levels, 8))
        for g in range(8):
            far = levels[np.abs(levels - a[p, g]) >= 10]
            a[p, g + 8] = far[np.random.randint(len(far))]
    return np.exp2(a.ravel()).repeat(32)


BF16 = ml_dtypes.bfloat16


def bf(x):
    return np.asarray(x, np.float32).astype(BF16)


def f64(x):
    return np.asarray(x).astype(np.float64)


M, DIN, D = 1024, 256, 1024


def setup_inputs():
    s = mx_kscale(D)
    s = s / s.max()
    r = np.random.standard_normal
    return {"S": bf(r((M, D)) * s),
            "X": bf(r((M, DIN))),
            "Uz": bf(r((DIN, D)) * 0.5 / np.sqrt(DIN)),
            "Ug": bf(r((DIN, D)) * 0.5 / np.sqrt(DIN)),
            "Ur": bf(r((DIN, D)) * 0.5 / np.sqrt(DIN)),
            "Uh": bf(r((DIN, D)) * 0.5 / np.sqrt(DIN)),
            "Wz": bf(r((D, D)) * 0.7 / np.sqrt(D) / s[:, None]),
            "Wg": bf(r((D, D)) * 0.7 / np.sqrt(D) / s[:, None]),
            "Wr": bf(r((D, D)) * 0.7 / np.sqrt(D) / s[:, None]),
            "Wh": bf(r((D, D)) * 1.0 / np.sqrt(D) / s[:, None]),
            "bz": bf(r((1, D)) * 0.3),
            "bg": bf(r((1, D)) * 0.3),
            "br": bf(r((1, D)) * 0.3),
            "bh": bf(r((1, D)) * 0.3)}


def reference(S, X, Uz, Ug, Ur, Uh, Wz, Wg, Wr, Wh, bz, bg, br, bh):
    Sf = f64(S)
    Sq = mxq(Sf, 1, "e4m3")
    Z = np.tanh(f64(X) @ f64(Uz) + (Sq @ mxq(f64(Wz), 0, "e4m3")) + f64(bz))
    G = np.tanh(f64(X) @ f64(Ug) + (Sq @ mxq(f64(Wg), 0, "e4m3")) + f64(bg))
    R = np.tanh(f64(X) @ f64(Ur) + (Sq @ mxq(f64(Wr), 0, "e4m3")) + f64(br))
    SR = Sf * R
    H = np.tanh(f64(X) @ f64(Uh) + (mxq(SR, 1, "e4m3") @ mxq(f64(Wh), 0, "e4m3")) + f64(bh))
    return (1.0 - G) * H + Z * Sf

@@ -1,0 +1,331 @@
+from contextlib import ExitStack
+
+import concourse.mybir as mybir
+from concourse.masks import make_identity
+
+F32 = mybir.dt.float32
+BF16 = mybir.dt.bfloat16
+U32 = mybir.dt.uint32
+U8 = mybir.dt.uint8
+FP8X4 = mybir.dt.float8_e4m3fn_x4
+ACT = mybir.ActivationFunctionType
+ALU = mybir.AluOpType
+
+P = 128
+PACK = 4
+K_PASS = P * PACK
+TOKENS = 1024
+D = 1024
+DIN = 256
+CHUNK = 512
+PASSES = D // K_PASS
+X_PASSES = DIN // P
+CHUNKS = TOKENS // CHUNK
+ROW_TILES = TOKENS // P
+ROWS_PER_CHUNK = CHUNK // P
+D_TILES = D // P
+HALVES = D // K_PASS
+GATES = ("r", "z", "g", "h")
+GROUP = PACK
+TILES_PER_GATE = HALVES * CHUNKS * GROUP
+GROUPS_PER_GATE = HALVES * CHUNKS
+N_TILES = len(GATES) * TILES_PER_GATE
+FIRST_H = GATES.index("h") * TILES_PER_GATE
+QUARTERS = len(GATES) * HALVES * PASSES
+AHEAD = 8
+QUARTERS_AHEAD = 3
+SR_LAG = 3
+TANH_LAG = 2
+FINISH_LAG = TANH_LAG + 1
+OUT_LAG = GROUP + FINISH_LAG + 2
+
+FLOPS = 2 * TOKENS * D * 4 * (D + DIN)
+
+
+def tile_lstmlayer_pa_kernel(tc, S, X, Uz, Ug, Ur, Uh, Wz, Wg, Wr, Wh, bz, bg, br, bh, out):
+    nc = tc.nc
+    u_dram = {"r": Ur, "z": Uz, "g": Ug, "h": Uh}
+    w_dram = {"r": Wr, "z": Wz, "g": Wg, "h": Wh}
+    b_dram = {"r": br, "z": bz, "g": bg, "h": bh}
+
+    with ExitStack() as ctx:
+        ctx.enter_context(tc.manual_schedule())
+        const = ctx.enter_context(tc.tile_pool(name="const", bufs=1))
+        keep = ctx.enter_context(tc.tile_pool(name="keep", bufs=1))
+        u_pool = ctx.enter_context(tc.tile_pool(name="u", bufs=2))
+        w_pool = ctx.enter_context(tc.tile_pool(name="w", bufs=2))
+        raw_pool = ctx.enter_context(tc.tile_pool(name="raw", bufs=3))
+        grouped_pool = ctx.enter_context(tc.tile_pool(name="grouped", bufs=2))
+        pre_pool = ctx.enter_context(tc.tile_pool(name="pre", bufs=AHEAD + FINISH_LAG + 2))
+
+        xT = keep.tile([P, X_PASSES, TOKENS], BF16)
+        sT = keep.tile([P, PASSES, TOKENS, PACK], BF16, align_bytes=64)
+        s_codes = keep.tile([P, PASSES, TOKENS], U32, align_bytes=64)
+        s_scales = keep.tile([P, PASSES, TOKENS], U8, align_bytes=64)
+        sr_codes = keep.tile([P, PASSES, TOKENS], U32, align_bytes=64)
+        sr_scales = keep.tile([P, PASSES, TOKENS], U8, align_bytes=64)
+        zs = keep.tile([P, D_TILES, TOKENS], F32)
+        rg_sb = keep.tile([P, D_TILES, TOKENS], F32)
+
+        u_sb = {}
+        raw = {}
+        grouped = {}
+        w_codes = {}
+        w_scales = {}
+        pre = {}
+        sr_tiles = {}
+
+        def copy_out(which, dest, source):
+            if which % 2 == 0:
+                nc.scalar.copy(out=dest, in_=source)
+            else:
+                nc.vector.tensor_copy(out=dest, in_=source)
+
+        def load_u(gate):
+            u_sb[gate] = u_pool.tile([P, X_PASSES, D], BF16, name="u_" + gate, tag="u")
+            nc.sync.dma_start(out=u_sb[gate][:], in_=u_dram[gate].rearrange("(x p) d -> p x d", p=P))
+
+        def load_weight_half(index):
+            gate, half = divmod(index, HALVES)
+            cols = slice(half * K_PASS, (half + 1) * K_PASS)
+            raw[index] = raw_pool.tile([P, PASSES, PACK, K_PASS], BF16, name="raw" + str(index), tag="raw")
+            for c in range(PASSES):
+                nc.sync.dma_start(
+                    out=raw[index][:, c, :, :],
+                    in_=w_dram[GATES[gate]][c * K_PASS : (c + 1) * K_PASS, cols].rearrange("(p t) d -> p t d", t=PACK),
+                )
+
+        def regroup_quarter(quarter):
+            index, c = divmod(quarter, PASSES)
+            gate = GATES[index // HALVES]
+            if quarter % (HALVES * PASSES) == 0:
+                w_codes[gate] = w_pool.tile([P, PASSES, D], U32, name="w_codes_" + gate, tag="w_codes", align_bytes=64)
+                w_scales[gate] = w_pool.tile([P, PASSES, D], U8, name="w_scales_" + gate, tag="w_scales", align_bytes=64)
+            grouped[quarter] = grouped_pool.tile(
+                [P, K_PASS, PACK], BF16, name="grouped" + str(quarter), tag="grouped", align_bytes=64
+            )
+            nc.vector.tensor_copy(
+                out=grouped[quarter][:].rearrange("p (i m) t -> p i m t", i=PACK),
+                in_=raw[index][:, c, :, :].rearrange("p t (m i) -> p i m t", i=PACK),
+            )
+            if c == PASSES - 1 and index + 3 < len(GATES) * HALVES:
+                load_weight_half(index + 3)
+
+        def quantise_quarter(quarter):
+            index, c = divmod(quarter, PASSES)
+            gate, half = divmod(index, HALVES)
+            cols = slice(half * K_PASS, (half + 1) * K_PASS)
+            nc.vector.quantize_mx(
+                out=w_codes[GATES[gate]][:, c, cols].bitcast(FP8X4),
+                scales=w_scales[GATES[gate]][:, c, cols],
+                in_=grouped[quarter][:].rearrange("p d t -> p (d t)"),
+            )
+
+        def where(n):
+            gate = GATES[n // TILES_PER_GATE]
+            half, rest = divmod(n % TILES_PER_GATE, CHUNKS * GROUP)
+            chunk, t = divmod(rest, GROUP)
+            return gate, half * PACK + t, slice(chunk * CHUNK, (chunk + 1) * CHUNK)
+
+        def plain_product(n, psum):
+            gate, j, tok = where(n)
+            xu_ps = psum.tile([P, CHUNK], F32, tag="plain")
+            for x in range(X_PASSES):
+                nc.tensor.matmul(
+                    out=xu_ps[:],
+                    lhsT=u_sb[gate][:, x, j // PACK * K_PASS + j % PACK : (j // PACK + 1) * K_PASS : PACK],
+                    rhs=xT[:, x, tok],
+                    start=(x == 0),
+                    stop=(x == X_PASSES - 1),
+                )
+            pre[n] = pre_pool.tile([P, CHUNK], F32, name="pre" + str(n), tag="pre")
+            nc.scalar.copy(out=pre[n][:], in_=xu_ps[:])
+            following = n // TILES_PER_GATE + 2
+            if n % TILES_PER_GATE == TILES_PER_GATE - 1 and following < len(GATES):
+                load_u(GATES[following])
+
+        def mx_product(n):
+            gate, j, tok = where(n)
+            a_codes, a_scales = (sr_codes, sr_scales) if gate == "h" else (s_codes, s_scales)
+            mx_ps = psum_mx.tile([P, CHUNK], F32)
+            for c in range(PASSES):
+                nc.tensor.matmul_mx(
+                    out=mx_ps[:],
+                    lhsT=w_codes[gate][:, c, j * P : (j + 1) * P].bitcast(FP8X4),
+                    lhsT_scale=w_scales[gate][:, c, j * P : (j + 1) * P],
+                    rhs=a_codes[:, c, tok].bitcast(FP8X4),
+                    rhs_scale=a_scales[:, c, tok],
+                    start=(c == 0),
+                    stop=(c == PASSES - 1),
+                )
+            column = j % PACK * len(GATES) * HALVES + GATES.index(gate) * HALVES + j // PACK
+            nc.vector.scalar_tensor_tensor(
+                out=pre[n][:],
+                in0=mx_ps[:],
+                scalar=bias_col[:, column : column + 1],
+                in1=pre[n][:],
+                op0=ALU.add,
+                op1=ALU.add,
+            )
+
+        def activate(n):
+            gate, j, tok = where(n)
+            group, t = divmod(n, GROUP)
+            if gate == "z":
+                dest = zs[:, j, tok]
+            elif gate == "h":
+                dest = pre[n][:]
+            else:
+                dest = rg_sb[:, j, tok]
+            nc.scalar.activation(out=dest, in_=pre[n][:], func=ACT.Tanh, scale=(-1.0 if gate == "g" else 1.0))
+            if gate == "r" and t == GROUP - 1:
+                sr_tiles[group] = sr_pool.tile([P, CHUNK, PACK], BF16, name="sr" + str(group), tag="sr", align_bytes=64)
+                r_group = rg_sb[:, j + 1 - PACK : j + 1, tok].rearrange("p t m -> p m t")
+                s_group = sT[:, j // PACK, tok, :]
+                for i in range(ROWS_PER_CHUNK):
+                    piece = slice(i * P, (i + 1) * P)
+                    nc.gpsimd.tensor_tensor(
+                        out=sr_tiles[group][:, piece, :], in0=r_group[:, piece, :], in1=s_group[:, piece, :], op=ALU.mult
+                    )
+            if gate == "z":
+                nc.gpsimd.tensor_tensor(out=dest, in0=dest, in1=sT[:, j // PACK, tok, j % PACK], op=ALU.mult)
+
+        def quantise_sr(group):
+            gate, j, tok = where(group * GROUP)
+            nc.vector.quantize_mx(
+                out=sr_codes[:, j // PACK, tok].bitcast(FP8X4),
+                scales=sr_scales[:, j // PACK, tok],
+                in_=sr_tiles[group][:].rearrange("p m t -> p (m t)"),
+            )
+
+        def combine(n):
+            gate, j, tok = where(n)
+            nc.vector.scalar_tensor_tensor(
+                out=rg_sb[:, j, tok], in0=rg_sb[:, j, tok], scalar=1.0, in1=pre[n][:], op0=ALU.add, op1=ALU.mult
+            )
+
+        def store_rows(group, i):
+            half, chunk = divmod(group, CHUNKS)
+            r = chunk * ROWS_PER_CHUNK + i
+            back_ps = psum_plain.tile([P, PACK, P], F32, tag="plain")
+            for t in range(PACK):
+                block = (slice(None), half * PACK + t, slice(r * P, (r + 1) * P))
+                nc.tensor.matmul(
+                    out=back_ps[:, t, :], lhsT=zs[block], rhs=ident_f32[:], is_transpose=True, start=True, stop=False
+                )
+                nc.tensor.matmul(
+                    out=back_ps[:, t, :], lhsT=rg_sb[block], rhs=ident_f32[:], is_transpose=True, start=False, stop=True
+                )
+            rows = rows_pool.tile([P, K_PASS], F32)
+            nc.scalar.copy(out=rows[:].rearrange("p (d t) -> p d t", t=PACK), in_=back_ps[:].rearrange("p t d -> p d t"))
+            nc.sync.dma_start(out=out[r * P : (r + 1) * P, half * K_PASS : (half + 1) * K_PASS], in_=rows[:])
+
+        with tc.tile_pool(name="natural", bufs=1) as natural, tc.psum_pool(
+            name="psum_in", bufs=5
+        ) as psum_in, tc.psum_pool(name="psum_first", bufs=3) as psum_first:
+            x_sb = natural.tile([P, ROW_TILES, DIN], BF16)
+            s_sb = natural.tile([P, ROW_TILES, D], BF16)
+            s_rows = S.rearrange("(r p) k -> p r k", p=P)
+            nc.sync.dma_start(out=x_sb[:], in_=X.rearrange("(r p) k -> p r k", p=P))
+            load_u("r")
+            nc.sync.dma_start(out=s_sb[:, :ROWS_PER_CHUNK, :], in_=s_rows[:, :ROWS_PER_CHUNK, :])
+            load_weight_half(0)
+            nc.sync.dma_start(out=s_sb[:, ROWS_PER_CHUNK:, :], in_=s_rows[:, ROWS_PER_CHUNK:, :])
+            load_weight_half(1)
+            load_u("z")
+            load_weight_half(2)
+
+            ident_bf16 = const.tile([P, P], BF16)
+            make_identity(nc, ident_bf16[:])
+            ident_f32 = const.tile([P, P], F32)
+            make_identity(nc, ident_f32[:])
+
+            bias_rows = const.tile([P, K_PASS], BF16)
+            nc.vector.memset(bias_rows[:], 0.0)
+            for i, gate in enumerate(GATES):
+                nc.scalar.dma_start(
+                    out=bias_rows[i * HALVES : (i + 1) * HALVES, :],
+                    in_=b_dram[gate].rearrange("o (h k) -> (o h) k", k=K_PASS),
+                )
+
+            warm = const.tile([P, 1], F32)
+            nc.vector.memset(warm[:], 0.0)
+            nc.scalar.activation(out=warm[:], in_=warm[:], func=ACT.Tanh)
+
+            for x in range(X_PASSES):
+                for chunk in range(CHUNKS):
+                    xt_ps = psum_in.tile([P, ROWS_PER_CHUNK, P], BF16, tag="in")
+                    for i in range(ROWS_PER_CHUNK):
+                        r = chunk * ROWS_PER_CHUNK + i
+                        nc.tensor.transpose(xt_ps[:, i, :], x_sb[:, r, x * P : (x + 1) * P], ident_bf16[:])
+                    copy_out(
+                        chunk, xT[:, x, chunk * CHUNK : (chunk + 1) * CHUNK], xt_ps[:].rearrange("p i m -> p (i m)")
+                    )
+
+            def transpose_s(chunk):
+                for c in range(PASSES):
+                    for i in range(ROWS_PER_CHUNK):
+                        r = chunk * ROWS_PER_CHUNK + i
+                        st_ps = psum_in.tile([P, PACK, P], BF16, tag="in")
+                        for t in range(PACK):
+                            columns = slice(c * K_PASS + t, (c + 1) * K_PASS, PACK)
+                            nc.tensor.transpose(st_ps[:, t, :], s_sb[:, r, columns], ident_bf16[:])
+                        copy_out(i if chunk == 0 else 0, sT[:, c, r * P : (r + 1) * P, :], st_ps[:].rearrange("p t m -> p m t"))
+
+            def quantise_s(chunk):
+                tok = slice(chunk * CHUNK, (chunk + 1) * CHUNK)
+                for c in range(PASSES):
+                    nc.vector.quantize_mx(
+                        out=s_codes[:, c, tok].bitcast(FP8X4),
+                        scales=s_scales[:, c, tok],
+                        in_=sT[:, c, tok, :].rearrange("p m t -> p (m t)"),
+                    )
+
+            for n in range(AHEAD // 2):
+                plain_product(n, psum_first)
+            transpose_s(0)
+            regroup_quarter(0)
+            quantise_s(0)
+            regroup_quarter(1)
+            quantise_quarter(0)
+            quantise_quarter(1)
+            for n in range(AHEAD // 2, AHEAD):
+                plain_product(n, psum_first)
+            transpose_s(1)
+            regroup_quarter(2)
+            quantise_s(1)
+
+            bias_ps = psum_in.tile([P, PACK, P], BF16, tag="in")
+            for t in range(PACK):
+                nc.tensor.transpose(bias_ps[:, t, :], bias_rows[:, t::PACK], ident_bf16[:])
+            bias_col = const.tile([P, PACK * len(GATES) * HALVES], F32)
+            nc.vector.tensor_copy(
+                out=bias_col[:].rearrange("p (t i) -> p t i", t=PACK), in_=bias_ps[:, :, : len(GATES) * HALVES]
+            )
+
+        psum_plain = ctx.enter_context(tc.psum_pool(name="psum_plain", bufs=5, reuse_waits="tile"))
+        psum_mx = ctx.enter_context(tc.psum_pool(name="psum_mx", bufs=3, reuse_waits="tile"))
+        sr_pool = ctx.enter_context(tc.tile_pool(name="sr", bufs=SR_LAG))
+        rows_pool = ctx.enter_context(tc.tile_pool(name="rows", bufs=4))
+
+        for n in range(N_TILES + OUT_LAG - 1):
+            group, t = divmod(n, GROUP)
+            if n + AHEAD < N_TILES:
+                plain_product(n + AHEAD, psum_plain)
+            if n < N_TILES:
+                mx_product(n)
+            if 0 <= n - TANH_LAG < N_TILES:
+                activate(n - TANH_LAG)
+            if FIRST_H <= n - FINISH_LAG < N_TILES:
+                combine(n - FINISH_LAG)
+            if t == 0:
+                if group + QUARTERS_AHEAD < QUARTERS:
+                    regroup_quarter(group + QUARTERS_AHEAD)
+                if group + QUARTERS_AHEAD - 1 < QUARTERS:
+                    quantise_quarter(group + QUARTERS_AHEAD - 1)
+                if 0 <= group - SR_LAG < GROUPS_PER_GATE:
+                    quantise_sr(group - SR_LAG)
+            pair, odd_step = divmod(n - FIRST_H - OUT_LAG, 2)
+            if pair >= 0 and odd_step == 0:
+                for i in range(2):
+                    store_rows(pair // 2, 2 * (pair % 2) + i)

@@ -22,22 +22,16 @@ PASSES = D // K_PASS
 X_PASSES = DIN // P
 CHUNKS = TOKENS // CHUNK
 ROW_TILES = TOKENS // P
-ROWS_PER_CHUNK = CHUNK // P
+ROWS = CHUNK // P
 D_TILES = D // P
 HALVES = D // K_PASS
 GATES = ("r", "z", "g", "h")
-GROUP = PACK
-TILES_PER_GATE = HALVES * CHUNKS * GROUP
 GROUPS_PER_GATE = HALVES * CHUNKS
-N_TILES = len(GATES) * TILES_PER_GATE
-FIRST_H = GATES.index("h") * TILES_PER_GATE
+N_GROUPS = len(GATES) * GROUPS_PER_GATE
+FIRST_Z = GATES.index("z") * GROUPS_PER_GATE
+FIRST_G = GATES.index("g") * GROUPS_PER_GATE
+FIRST_H = GATES.index("h") * GROUPS_PER_GATE
 QUARTERS = len(GATES) * HALVES * PASSES
-AHEAD = 8
-QUARTERS_AHEAD = 3
-SR_LAG = 3
-TANH_LAG = 2
-FINISH_LAG = TANH_LAG + 1
-OUT_LAG = GROUP + FINISH_LAG + 2
 
 FLOPS = 2 * TOKENS * D * 4 * (D + DIN)
 
@@ -46,37 +40,42 @@ def tile_lstmlayer_pa_kernel(tc, S, X, Uz, Ug, Ur, Uh, Wz, Wg, Wr, Wh, bz, bg, b
     nc = tc.nc
     u_dram = {"r": Ur, "z": Uz, "g": Ug, "h": Uh}
     w_dram = {"r": Wr, "z": Wz, "g": Wg, "h": Wh}
-    b_dram = {"r": br, "z": bz, "g": bg, "h": bh}
+    b_dram = {"z": bz, "g": bg, "h": bh}
 
     with ExitStack() as ctx:
         ctx.enter_context(tc.manual_schedule())
-        const = ctx.enter_context(tc.tile_pool(name="const", bufs=1))
         keep = ctx.enter_context(tc.tile_pool(name="keep", bufs=1))
-        u_pool = ctx.enter_context(tc.tile_pool(name="u", bufs=2))
+        u_pool = ctx.enter_context(tc.tile_pool(name="u", bufs=3))
         w_pool = ctx.enter_context(tc.tile_pool(name="w", bufs=2))
         raw_pool = ctx.enter_context(tc.tile_pool(name="raw", bufs=3))
         grouped_pool = ctx.enter_context(tc.tile_pool(name="grouped", bufs=2))
-        pre_pool = ctx.enter_context(tc.tile_pool(name="pre", bufs=AHEAD + FINISH_LAG + 2))
+        sr_pool = ctx.enter_context(tc.tile_pool(name="sr", bufs=2))
+        copied_pool = ctx.enter_context(tc.tile_pool(name="copied", bufs=8))
+        h_pool = ctx.enter_context(tc.tile_pool(name="h", bufs=4))
+        psum = ctx.enter_context(tc.psum_pool(name="psum", bufs=4, reuse_waits="tile"))
 
+        x_sb = keep.tile([P, ROW_TILES, DIN], BF16)
+        s_sb = keep.tile([P, ROW_TILES, D], BF16, align_bytes=64)
         xT = keep.tile([P, X_PASSES, TOKENS], BF16)
         sT = keep.tile([P, PASSES, TOKENS, PACK], BF16, align_bytes=64)
         s_codes = keep.tile([P, PASSES, TOKENS], U32, align_bytes=64)
         s_scales = keep.tile([P, PASSES, TOKENS], U8, align_bytes=64)
         sr_codes = keep.tile([P, PASSES, TOKENS], U32, align_bytes=64)
         sr_scales = keep.tile([P, PASSES, TOKENS], U8, align_bytes=64)
-        zs = keep.tile([P, D_TILES, TOKENS], F32)
-        rg_sb = keep.tile([P, D_TILES, TOKENS], F32)
+        slots = GROUPS_PER_GATE * PACK
+        zs = keep.tile([P, slots, CHUNK], F32)
+        rg = keep.tile([P, slots, CHUNK], F32)
 
         u_sb = {}
         raw = {}
         grouped = {}
         w_codes = {}
         w_scales = {}
-        pre = {}
+        copied = {}
         sr_tiles = {}
 
-        def copy_out(which, dest, source):
-            if which % 2 == 0:
+        def copy_on(engine, dest, source):
+            if engine == "scalar":
                 nc.scalar.copy(out=dest, in_=source)
             else:
                 nc.vector.tensor_copy(out=dest, in_=source)
@@ -95,7 +94,7 @@ def tile_lstmlayer_pa_kernel(tc, S, X, Uz, Ug, Ur, Uh, Wz, Wg, Wr, Wh, bz, bg, b
                     in_=w_dram[GATES[gate]][c * K_PASS : (c + 1) * K_PASS, cols].rearrange("(p t) d -> p t d", t=PACK),
                 )
 
-        def regroup_quarter(quarter):
+        def regroup_quarter(quarter, engine):
             index, c = divmod(quarter, PASSES)
             gate = GATES[index // HALVES]
             if quarter % (HALVES * PASSES) == 0:
@@ -104,10 +103,14 @@ def tile_lstmlayer_pa_kernel(tc, S, X, Uz, Ug, Ur, Uh, Wz, Wg, Wr, Wh, bz, bg, b
             grouped[quarter] = grouped_pool.tile(
                 [P, K_PASS, PACK], BF16, name="grouped" + str(quarter), tag="grouped", align_bytes=64
             )
-            nc.vector.tensor_copy(
-                out=grouped[quarter][:].rearrange("p (i m) t -> p i m t", i=PACK),
-                in_=raw[index][:, c, :, :].rearrange("p t (m i) -> p i m t", i=PACK),
-            )
+            source = raw[index][:, c, :, :]
+            if gate == "r":
+                dest = grouped[quarter][:].rearrange("p (i m) t -> p i m t", i=PACK)
+                source = source.rearrange("p t (m i) -> p i m t", i=PACK)
+            else:
+                dest = grouped[quarter][:].rearrange("p (q i) t -> p q t i", i=4)
+                source = source.rearrange("p t (q i) -> p q t i", i=4)
+            copy_on(engine, dest, source)
             if c == PASSES - 1 and index + 3 < len(GATES) * HALVES:
                 load_weight_half(index + 3)
 
@@ -121,211 +124,235 @@ def tile_lstmlayer_pa_kernel(tc, S, X, Uz, Ug, Ur, Uh, Wz, Wg, Wr, Wh, bz, bg, b
                 in_=grouped[quarter][:].rearrange("p d t -> p (d t)"),
             )
 
-        def where(n):
-            gate = GATES[n // TILES_PER_GATE]
-            half, rest = divmod(n % TILES_PER_GATE, CHUNKS * GROUP)
-            chunk, t = divmod(rest, GROUP)
-            return gate, half * PACK + t, slice(chunk * CHUNK, (chunk + 1) * CHUNK)
+        def where(m):
+            gate, g = divmod(m, GROUPS_PER_GATE)
+            half, chunk = divmod(g, CHUNKS)
+            return GATES[gate], half, chunk, slice(chunk * CHUNK, (chunk + 1) * CHUNK), g * PACK
 
-        def plain_product(n, psum):
-            gate, j, tok = where(n)
-            xu_ps = psum.tile([P, CHUNK], F32, tag="plain")
+        def plain_r(n, engine):
+            g, t = divmod(n, PACK)
+            gate, half, chunk, tok, slot = where(g)
+            ps = psum.tile([P, CHUNK], F32, name="xr" + str(n), tag="b")
             for x in range(X_PASSES):
                 nc.tensor.matmul(
-                    out=xu_ps[:],
-                    lhsT=u_sb[gate][:, x, j // PACK * K_PASS + j % PACK : (j // PACK + 1) * K_PASS : PACK],
+                    out=ps[:],
+                    lhsT=u_sb["r"][:, x, half * K_PASS + t : (half + 1) * K_PASS : PACK],
                     rhs=xT[:, x, tok],
                     start=(x == 0),
                     stop=(x == X_PASSES - 1),
                 )
-            pre[n] = pre_pool.tile([P, CHUNK], F32, name="pre" + str(n), tag="pre")
-            nc.scalar.copy(out=pre[n][:], in_=xu_ps[:])
-            following = n // TILES_PER_GATE + 2
-            if n % TILES_PER_GATE == TILES_PER_GATE - 1 and following < len(GATES):
-                load_u(GATES[following])
+            copy_on(engine, rg[:, slot + t, :], ps[:])
 
-        def mx_product(n):
-            gate, j, tok = where(n)
+        def mx_tile(m, t):
+            gate, half, chunk, tok, slot = where(m)
             a_codes, a_scales = (sr_codes, sr_scales) if gate == "h" else (s_codes, s_scales)
-            mx_ps = psum_mx.tile([P, CHUNK], F32)
+            cols = slice(half * K_PASS + t * P, half * K_PASS + (t + 1) * P)
+            ps = psum.tile([P, CHUNK], F32, name="mx" + str(m) + "_" + str(t), tag="a")
             for c in range(PASSES):
                 nc.tensor.matmul_mx(
-                    out=mx_ps[:],
-                    lhsT=w_codes[gate][:, c, j * P : (j + 1) * P].bitcast(FP8X4),
-                    lhsT_scale=w_scales[gate][:, c, j * P : (j + 1) * P],
+                    out=ps[:],
+                    lhsT=w_codes[gate][:, c, cols].bitcast(FP8X4),
+                    lhsT_scale=w_scales[gate][:, c, cols],
                     rhs=a_codes[:, c, tok].bitcast(FP8X4),
                     rhs_scale=a_scales[:, c, tok],
                     start=(c == 0),
                     stop=(c == PASSES - 1),
                 )
-            column = j % PACK * len(GATES) * HALVES + GATES.index(gate) * HALVES + j // PACK
-            nc.vector.scalar_tensor_tensor(
-                out=pre[n][:],
-                in0=mx_ps[:],
-                scalar=bias_col[:, column : column + 1],
-                in1=pre[n][:],
-                op0=ALU.add,
-                op1=ALU.add,
-            )
+            return ps
 
-        def activate(n):
-            gate, j, tok = where(n)
-            group, t = divmod(n, GROUP)
-            if gate == "z":
-                dest = zs[:, j, tok]
-            elif gate == "h":
-                dest = pre[n][:]
-            else:
-                dest = rg_sb[:, j, tok]
-            nc.scalar.activation(out=dest, in_=pre[n][:], func=ACT.Tanh, scale=(-1.0 if gate == "g" else 1.0))
-            if gate == "r" and t == GROUP - 1:
-                sr_tiles[group] = sr_pool.tile([P, CHUNK, PACK], BF16, name="sr" + str(group), tag="sr", align_bytes=64)
-                r_group = rg_sb[:, j + 1 - PACK : j + 1, tok].rearrange("p t m -> p m t")
-                s_group = sT[:, j // PACK, tok, :]
-                for i in range(ROWS_PER_CHUNK):
-                    piece = slice(i * P, (i + 1) * P)
-                    nc.gpsimd.tensor_tensor(
-                        out=sr_tiles[group][:, piece, :], in0=r_group[:, piece, :], in1=s_group[:, piece, :], op=ALU.mult
-                    )
-            if gate == "z":
-                nc.gpsimd.tensor_tensor(out=dest, in0=dest, in1=sT[:, j // PACK, tok, j % PACK], op=ALU.mult)
-
-        def quantise_sr(group):
-            gate, j, tok = where(group * GROUP)
-            nc.vector.quantize_mx(
-                out=sr_codes[:, j // PACK, tok].bitcast(FP8X4),
-                scales=sr_scales[:, j // PACK, tok],
-                in_=sr_tiles[group][:].rearrange("p m t -> p (m t)"),
-            )
-
-        def combine(n):
-            gate, j, tok = where(n)
-            nc.vector.scalar_tensor_tensor(
-                out=rg_sb[:, j, tok], in0=rg_sb[:, j, tok], scalar=1.0, in1=pre[n][:], op0=ALU.add, op1=ALU.mult
-            )
-
-        def store_rows(group, i):
-            half, chunk = divmod(group, CHUNKS)
-            r = chunk * ROWS_PER_CHUNK + i
-            back_ps = psum_plain.tile([P, PACK, P], F32, tag="plain")
+        def mx_group_r(m):
+            gate, half, chunk, tok, slot = where(m)
             for t in range(PACK):
-                block = (slice(None), half * PACK + t, slice(r * P, (r + 1) * P))
-                nc.tensor.matmul(
-                    out=back_ps[:, t, :], lhsT=zs[block], rhs=ident_f32[:], is_transpose=True, start=True, stop=False
+                ps = mx_tile(m, t)
+                place = rg[:, slot + t, :]
+                nc.vector.scalar_tensor_tensor(
+                    out=place, in0=ps[:], scalar=br_col[:, half, t : t + 1], in1=place, op0=ALU.add, op1=ALU.add
                 )
-                nc.tensor.matmul(
-                    out=back_ps[:, t, :], lhsT=rg_sb[block], rhs=ident_f32[:], is_transpose=True, start=False, stop=True
-                )
-            rows = rows_pool.tile([P, K_PASS], F32)
-            nc.scalar.copy(out=rows[:].rearrange("p (d t) -> p d t", t=PACK), in_=back_ps[:].rearrange("p t d -> p d t"))
-            nc.sync.dma_start(out=out[r * P : (r + 1) * P, half * K_PASS : (half + 1) * K_PASS], in_=rows[:])
+            for t in range(PACK):
+                nc.scalar.activation(out=rg[:, slot + t, :], in_=rg[:, slot + t, :], func=ACT.Tanh)
 
-        with tc.tile_pool(name="natural", bufs=1) as natural, tc.psum_pool(
-            name="psum_in", bufs=5
-        ) as psum_in, tc.psum_pool(name="psum_first", bufs=3) as psum_first:
-            x_sb = natural.tile([P, ROW_TILES, DIN], BF16)
-            s_sb = natural.tile([P, ROW_TILES, D], BF16)
-            s_rows = S.rearrange("(r p) k -> p r k", p=P)
-            nc.sync.dma_start(out=x_sb[:], in_=X.rearrange("(r p) k -> p r k", p=P))
-            load_u("r")
-            nc.sync.dma_start(out=s_sb[:, :ROWS_PER_CHUNK, :], in_=s_rows[:, :ROWS_PER_CHUNK, :])
-            load_weight_half(0)
-            nc.sync.dma_start(out=s_sb[:, ROWS_PER_CHUNK:, :], in_=s_rows[:, ROWS_PER_CHUNK:, :])
-            load_weight_half(1)
-            load_u("z")
-            load_weight_half(2)
+        def mx_group(m):
+            gate, half, chunk, tok, slot = where(m)
+            copied[m] = []
+            for t in range(PACK):
+                ps = mx_tile(m, t)
+                tile = copied_pool.tile([P, CHUNK], F32, name="copied" + str(m) + "_" + str(t), tag="copied")
+                column = (GATES.index(gate) - 1) * D_TILES + half * PACK + t
+                nc.scalar.activation(out=tile[:], in_=ps[:], func=ACT.Identity, bias=bias_col[:, column : column + 1])
+                copied[m].append(tile)
 
-            ident_bf16 = const.tile([P, P], BF16)
-            make_identity(nc, ident_bf16[:])
-            ident_f32 = const.tile([P, P], F32)
-            make_identity(nc, ident_f32[:])
-
-            bias_rows = const.tile([P, K_PASS], BF16)
-            nc.vector.memset(bias_rows[:], 0.0)
-            for i, gate in enumerate(GATES):
-                nc.scalar.dma_start(
-                    out=bias_rows[i * HALVES : (i + 1) * HALVES, :],
-                    in_=b_dram[gate].rearrange("o (h k) -> (o h) k", k=K_PASS),
-                )
-
-            warm = const.tile([P, 1], F32)
-            nc.vector.memset(warm[:], 0.0)
-            nc.scalar.activation(out=warm[:], in_=warm[:], func=ACT.Tanh)
-
-            for x in range(X_PASSES):
-                for chunk in range(CHUNKS):
-                    xt_ps = psum_in.tile([P, ROWS_PER_CHUNK, P], BF16, tag="in")
-                    for i in range(ROWS_PER_CHUNK):
-                        r = chunk * ROWS_PER_CHUNK + i
-                        nc.tensor.transpose(xt_ps[:, i, :], x_sb[:, r, x * P : (x + 1) * P], ident_bf16[:])
-                    copy_out(
-                        chunk, xT[:, x, chunk * CHUNK : (chunk + 1) * CHUNK], xt_ps[:].rearrange("p i m -> p (i m)")
-                    )
-
-            def transpose_s(chunk):
-                for c in range(PASSES):
-                    for i in range(ROWS_PER_CHUNK):
-                        r = chunk * ROWS_PER_CHUNK + i
-                        st_ps = psum_in.tile([P, PACK, P], BF16, tag="in")
+        def sum_group(m):
+            gate, half, chunk, tok, slot = where(m)
+            for i in range(ROWS):
+                r = chunk * ROWS + i
+                rows = slice(r * P, (r + 1) * P)
+                ps = psum.tile([P, K_PASS], F32, name="sum" + str(m) + "_" + str(i), tag="b")
+                for x in range(X_PASSES):
+                    if x == X_PASSES - 1:
                         for t in range(PACK):
-                            columns = slice(c * K_PASS + t, (c + 1) * K_PASS, PACK)
-                            nc.tensor.transpose(st_ps[:, t, :], s_sb[:, r, columns], ident_bf16[:])
-                        copy_out(i if chunk == 0 else 0, sT[:, c, r * P : (r + 1) * P, :], st_ps[:].rearrange("p t m -> p m t"))
-
-            def quantise_s(chunk):
-                tok = slice(chunk * CHUNK, (chunk + 1) * CHUNK)
-                for c in range(PASSES):
-                    nc.vector.quantize_mx(
-                        out=s_codes[:, c, tok].bitcast(FP8X4),
-                        scales=s_scales[:, c, tok],
-                        in_=sT[:, c, tok, :].rearrange("p m t -> p (m t)"),
+                            nc.tensor.matmul(
+                                out=ps[:, t * P : (t + 1) * P],
+                                lhsT=copied[m][t][:, i * P : (i + 1) * P],
+                                rhs=ident_f32[:],
+                                is_transpose=True,
+                                start=False,
+                                stop=False,
+                            )
+                    nc.tensor.matmul(
+                        out=ps[:],
+                        lhsT=xT[:, x, rows],
+                        rhs=u_sb[gate][:, x, half * K_PASS : (half + 1) * K_PASS],
+                        start=(x == 0),
+                        stop=(x == X_PASSES - 1),
                     )
+                if gate == "z":
+                    nc.scalar.activation(out=zs[:, slot + i, :], in_=ps[:], func=ACT.Tanh)
+                elif gate == "g":
+                    nc.scalar.activation(out=rg[:, slot + i, :], in_=ps[:], func=ACT.Tanh, scale=-1.0)
+                else:
+                    h = h_pool.tile([P, K_PASS], F32, name="h" + str(m) + "_" + str(i), tag="h")
+                    nc.scalar.activation(out=h[:], in_=ps[:], func=ACT.Tanh)
+                    nc.vector.scalar_tensor_tensor(
+                        out=h[:], in0=rg[:, slot + i, :], scalar=1.0, in1=h[:], op0=ALU.add, op1=ALU.mult
+                    )
+                    nc.vector.tensor_tensor(out=h[:], in0=h[:], in1=zs[:, slot + i, :], op=ALU.add)
+                    nc.sync.dma_start(out=out[rows, half * K_PASS : (half + 1) * K_PASS], in_=h[:])
 
-            for n in range(AHEAD // 2):
-                plain_product(n, psum_first)
-            transpose_s(0)
-            regroup_quarter(0)
-            quantise_s(0)
-            regroup_quarter(1)
-            quantise_quarter(0)
-            quantise_quarter(1)
-            for n in range(AHEAD // 2, AHEAD):
-                plain_product(n, psum_first)
-            transpose_s(1)
-            regroup_quarter(2)
-            quantise_s(1)
-
-            bias_ps = psum_in.tile([P, PACK, P], BF16, tag="in")
-            for t in range(PACK):
-                nc.tensor.transpose(bias_ps[:, t, :], bias_rows[:, t::PACK], ident_bf16[:])
-            bias_col = const.tile([P, PACK * len(GATES) * HALVES], F32)
-            nc.vector.tensor_copy(
-                out=bias_col[:].rearrange("p (t i) -> p t i", t=PACK), in_=bias_ps[:, :, : len(GATES) * HALVES]
+        def multiply_sr(g):
+            gate, half, chunk, tok, slot = where(g)
+            sr_tiles[g] = sr_pool.tile([P, CHUNK, PACK], BF16, name="sr" + str(g), tag="sr", align_bytes=64)
+            nc.vector.tensor_tensor(
+                out=sr_tiles[g][:],
+                in0=rg[:, slot : slot + PACK, :].rearrange("p t m -> p m t"),
+                in1=sT[:, half, tok, :],
+                op=ALU.mult,
             )
 
-        psum_plain = ctx.enter_context(tc.psum_pool(name="psum_plain", bufs=5, reuse_waits="tile"))
-        psum_mx = ctx.enter_context(tc.psum_pool(name="psum_mx", bufs=3, reuse_waits="tile"))
-        sr_pool = ctx.enter_context(tc.tile_pool(name="sr", bufs=SR_LAG))
-        rows_pool = ctx.enter_context(tc.tile_pool(name="rows", bufs=4))
+        def quantise_sr(g):
+            gate, half, chunk, tok, slot = where(g)
+            nc.vector.quantize_mx(
+                out=sr_codes[:, half, tok].bitcast(FP8X4),
+                scales=sr_scales[:, half, tok],
+                in_=sr_tiles[g][:].rearrange("p m t -> p (m t)"),
+            )
 
-        for n in range(N_TILES + OUT_LAG - 1):
-            group, t = divmod(n, GROUP)
-            if n + AHEAD < N_TILES:
-                plain_product(n + AHEAD, psum_plain)
-            if n < N_TILES:
-                mx_product(n)
-            if 0 <= n - TANH_LAG < N_TILES:
-                activate(n - TANH_LAG)
-            if FIRST_H <= n - FINISH_LAG < N_TILES:
-                combine(n - FINISH_LAG)
-            if t == 0:
-                if group + QUARTERS_AHEAD < QUARTERS:
-                    regroup_quarter(group + QUARTERS_AHEAD)
-                if group + QUARTERS_AHEAD - 1 < QUARTERS:
-                    quantise_quarter(group + QUARTERS_AHEAD - 1)
-                if 0 <= group - SR_LAG < GROUPS_PER_GATE:
-                    quantise_sr(group - SR_LAG)
-            pair, odd_step = divmod(n - FIRST_H - OUT_LAG, 2)
-            if pair >= 0 and odd_step == 0:
-                for i in range(2):
-                    store_rows(pair // 2, 2 * (pair % 2) + i)
+        def multiply_zs(g):
+            gate, half, chunk, tok, slot = where(g)
+            for i in range(ROWS):
+                place = zs[:, slot + i, :]
+                s_part = s_sb[:, chunk * ROWS + i, half * K_PASS : (half + 1) * K_PASS]
+                nc.vector.tensor_tensor(out=place, in0=place, in1=s_part, op=ALU.mult)
+
+        s_rows = S.rearrange("(r p) k -> p r k", p=P)
+        nc.sync.dma_start(out=x_sb[:], in_=X.rearrange("(r p) k -> p r k", p=P))
+        load_u("r")
+        nc.sync.dma_start(out=s_sb[:, :ROWS, :], in_=s_rows[:, :ROWS, :])
+        load_weight_half(0)
+        nc.sync.dma_start(out=s_sb[:, ROWS:, :], in_=s_rows[:, ROWS:, :])
+        load_weight_half(1)
+        load_weight_half(2)
+        load_u("z")
+        load_u("g")
+
+        ident_bf16 = keep.tile([P, P], BF16)
+        make_identity(nc, ident_bf16[:])
+        ident_f32 = keep.tile([P, P], F32)
+        make_identity(nc, ident_f32[:])
+
+        bias_rows = keep.tile([P, P], BF16)
+        nc.vector.memset(bias_rows[:], 0.0)
+        for i, gate in enumerate(GATES[1:]):
+            nc.scalar.dma_start(
+                out=bias_rows[i * D_TILES : (i + 1) * D_TILES, :],
+                in_=b_dram[gate].rearrange("o (j p) -> (o j) p", p=P),
+            )
+        br_col = keep.tile([P, HALVES, PACK], BF16)
+        nc.scalar.dma_start(out=br_col[:], in_=br.rearrange("o (h p t) -> p (o h) t", p=P, t=PACK))
+
+        warm = keep.tile([P, 1], F32)
+        nc.vector.memset(warm[:], 0.0)
+        nc.scalar.activation(out=warm[:], in_=warm[:], func=ACT.Tanh)
+
+        for chunk in range(CHUNKS):
+            for x in range(X_PASSES):
+                ps = psum.tile([P, ROWS, P], BF16, name="xt" + str(chunk) + str(x), tag="b")
+                for i in range(ROWS):
+                    nc.tensor.transpose(ps[:, i, :], x_sb[:, chunk * ROWS + i, x * P : (x + 1) * P], ident_bf16[:])
+                copy_on(
+                    "vector" if x == 0 else "scalar",
+                    xT[:, x, chunk * CHUNK : (chunk + 1) * CHUNK],
+                    ps[:].rearrange("p i m -> p (i m)"),
+                )
+
+        s_words = s_sb[:].rearrange("p r k -> p (r k)").bitcast(F32)
+        sT_words = sT[:].rearrange("p c m t -> p (c m t)").bitcast(F32)
+
+        def transpose_s(chunk, engines):
+            for c in range(PASSES):
+                for pair in range(ROWS // 2):
+                    r0 = chunk * ROWS + pair * 2
+                    ps = psum.tile([P, 2, 2, P], F32, name="st" + str(r0) + str(c), tag="a")
+                    for i in range(2):
+                        start = (r0 + i) * (D // 2) + c * (K_PASS // 2)
+                        for u in range(2):
+                            nc.tensor.transpose(
+                                ps[:, i, u, :], s_words[:, start + u : start + K_PASS // 2 : 2], ident_f32[:]
+                            )
+                    first = (c * TOKENS + r0 * P) * 2
+                    copy_on(
+                        engines[c],
+                        sT_words[:, first : first + 4 * P].rearrange("p (i m u) -> p i m u", i=2, u=2),
+                        ps[:].rearrange("p i u m -> p i m u"),
+                    )
+
+        def quantise_s(chunk, c):
+            tok = slice(chunk * CHUNK, (chunk + 1) * CHUNK)
+            nc.vector.quantize_mx(
+                out=s_codes[:, c, tok].bitcast(FP8X4),
+                scales=s_scales[:, c, tok],
+                in_=sT[:, c, tok, :].rearrange("p m t -> p (m t)"),
+            )
+
+        for n in range(0, 4):
+            plain_r(n, "scalar" if n % 2 == 0 else "vector")
+        transpose_s(0, ("vector", "scalar"))
+        for n in range(4, 8):
+            plain_r(n, "scalar")
+        regroup_quarter(0, "vector")
+        quantise_s(0, 0)
+        regroup_quarter(1, "vector")
+        quantise_s(0, 1)
+        quantise_quarter(0)
+        quantise_quarter(1)
+        for n in range(8, 12):
+            plain_r(n, "scalar")
+        transpose_s(1, ("scalar", "scalar"))
+        for n in range(12, 16):
+            plain_r(n, "scalar")
+        bias_ps = psum.tile([P, P], BF16, name="bias_ps", tag="a")
+        nc.tensor.transpose(bias_ps[:], bias_rows[:], ident_bf16[:])
+        bias_col = keep.tile([P, (len(GATES) - 1) * D_TILES], F32)
+        nc.scalar.copy(out=bias_col[:], in_=bias_ps[:, : (len(GATES) - 1) * D_TILES])
+        regroup_quarter(2, "scalar")
+        quantise_s(1, 0)
+        quantise_s(1, 1)
+
+        for m in range(N_GROUPS + 1):
+            if m < FIRST_Z:
+                mx_group_r(m)
+            elif m < N_GROUPS:
+                mx_group(m)
+            if m - 1 >= FIRST_Z:
+                sum_group(m - 1)
+            if m + 2 < QUARTERS:
+                quantise_quarter(m + 2)
+            if m + 3 < QUARTERS:
+                regroup_quarter(m + 3, "scalar" if m == 0 else "vector")
+            if m == 2:
+                load_u("h")
+            if 0 <= m - FIRST_Z - 2 < GROUPS_PER_GATE:
+                quantise_sr(m - FIRST_Z - 2)
+            if 0 <= m - FIRST_Z < GROUPS_PER_GATE:
+                multiply_sr(m - FIRST_Z)
+            if 0 <= m - FIRST_G < GROUPS_PER_GATE:
+                multiply_zs(m - FIRST_G)

@@ -183,28 +183,29 @@ def tile_lstmlayer_pa_kernel(tc, S, X, Uz, Ug, Ur, Uh, Wz, Wg, Wr, Wh, bz, bg, b
 
         def sum_group(m):
             gate, half, chunk, tok, slot = where(m)
+            sums = [psum.tile([P, K_PASS], F32, name="sum" + str(m) + "_" + str(i), tag="b") for i in range(ROWS)]
             for i in range(ROWS):
-                r = chunk * ROWS + i
-                rows = slice(r * P, (r + 1) * P)
-                ps = psum.tile([P, K_PASS], F32, name="sum" + str(m) + "_" + str(i), tag="b")
                 for x in range(X_PASSES):
-                    if x == X_PASSES - 1:
-                        for t in range(PACK):
-                            nc.tensor.matmul(
-                                out=ps[:, t * P : (t + 1) * P],
-                                lhsT=copied[m][t][:, i * P : (i + 1) * P],
-                                rhs=ident_f32[:],
-                                is_transpose=True,
-                                start=False,
-                                stop=False,
-                            )
                     nc.tensor.matmul(
-                        out=ps[:],
-                        lhsT=xT[:, x, rows],
+                        out=sums[i][:],
+                        lhsT=xT[:, x, (chunk * ROWS + i) * P : (chunk * ROWS + i + 1) * P],
                         rhs=u_sb[gate][:, x, half * K_PASS : (half + 1) * K_PASS],
                         start=(x == 0),
-                        stop=(x == X_PASSES - 1),
+                        stop=False,
                     )
+            for i in range(ROWS):
+                ps = sums[i]
+                for t in range(PACK):
+                    nc.tensor.matmul(
+                        out=ps[:, t * P : (t + 1) * P],
+                        lhsT=copied[m][t][:, i * P : (i + 1) * P],
+                        rhs=ident_f32[:],
+                        is_transpose=True,
+                        start=False,
+                        stop=(t == PACK - 1),
+                    )
+                r = chunk * ROWS + i
+                rows = slice(r * P, (r + 1) * P)
                 if gate == "z":
                     nc.scalar.activation(out=zs[:, slot + i, :], in_=ps[:], func=ACT.Tanh)
                 elif gate == "g":

@@ -27,11 +27,13 @@ D_TILES = D // P
 HALVES = D // K_PASS
 GATES = ("r", "z", "g", "h")
 GROUPS_PER_GATE = HALVES * CHUNKS
-N_GROUPS = len(GATES) * GROUPS_PER_GATE
-FIRST_Z = GATES.index("z") * GROUPS_PER_GATE
-FIRST_G = GATES.index("g") * GROUPS_PER_GATE
-FIRST_H = GATES.index("h") * GROUPS_PER_GATE
-QUARTERS = len(GATES) * HALVES * PASSES
+ORDER = (("r", 0), ("z", 0), ("r", 1), ("z", 1), ("g", 0), ("g", 1), ("h", 0), ("h", 1))
+N_GROUPS = len(ORDER) * CHUNKS
+QUARTERS = len(ORDER) * PASSES
+
+SR_FORMED = {3: 0, 4: 1, 6: 2, 7: 3}
+SR_QUANTISED = {5: 0, 6: 1, 8: 2, 9: 3}
+ZS_FORMED = {8: 0, 9: 1, 10: 2, 11: 3}
 
 FLOPS = 2 * TOKENS * D * 4 * (D + DIN)
 
@@ -85,21 +87,18 @@ def tile_lstmlayer_pa_kernel(tc, S, X, Uz, Ug, Ur, Uh, Wz, Wg, Wr, Wh, bz, bg, b
             nc.sync.dma_start(out=u_sb[gate][:], in_=u_dram[gate].rearrange("(x p) d -> p x d", p=P))
 
         def load_weight_half(index):
-            gate, half = divmod(index, HALVES)
+            gate, half = ORDER[index]
             cols = slice(half * K_PASS, (half + 1) * K_PASS)
             raw[index] = raw_pool.tile([P, PASSES, PACK, K_PASS], BF16, name="raw" + str(index), tag="raw")
             for c in range(PASSES):
                 nc.sync.dma_start(
                     out=raw[index][:, c, :, :],
-                    in_=w_dram[GATES[gate]][c * K_PASS : (c + 1) * K_PASS, cols].rearrange("(p t) d -> p t d", t=PACK),
+                    in_=w_dram[gate][c * K_PASS : (c + 1) * K_PASS, cols].rearrange("(p t) d -> p t d", t=PACK),
                 )
 
         def regroup_quarter(quarter, engine):
             index, c = divmod(quarter, PASSES)
-            gate = GATES[index // HALVES]
-            if quarter % (HALVES * PASSES) == 0:
-                w_codes[gate] = w_pool.tile([P, PASSES, D], U32, name="w_codes_" + gate, tag="w_codes", align_bytes=64)
-                w_scales[gate] = w_pool.tile([P, PASSES, D], U8, name="w_scales_" + gate, tag="w_scales", align_bytes=64)
+            gate = ORDER[index][0]
             grouped[quarter] = grouped_pool.tile(
                 [P, K_PASS, PACK], BF16, name="grouped" + str(quarter), tag="grouped", align_bytes=64
             )
@@ -111,27 +110,34 @@ def tile_lstmlayer_pa_kernel(tc, S, X, Uz, Ug, Ur, Uh, Wz, Wg, Wr, Wh, bz, bg, b
                 dest = grouped[quarter][:].rearrange("p (q i) t -> p q t i", i=4)
                 source = source.rearrange("p t (q i) -> p q t i", i=4)
             copy_on(engine, dest, source)
-            if c == PASSES - 1 and index + 3 < len(GATES) * HALVES:
+            if c == PASSES - 1 and index + 3 < len(ORDER):
                 load_weight_half(index + 3)
 
         def quantise_quarter(quarter):
             index, c = divmod(quarter, PASSES)
-            gate, half = divmod(index, HALVES)
+            gate, half = ORDER[index]
             cols = slice(half * K_PASS, (half + 1) * K_PASS)
+            if gate not in w_codes:
+                w_codes[gate] = w_pool.tile([P, PASSES, D], U32, name="w_codes_" + gate, tag="w_codes", align_bytes=64)
+                w_scales[gate] = w_pool.tile([P, PASSES, D], U8, name="w_scales_" + gate, tag="w_scales", align_bytes=64)
             nc.vector.quantize_mx(
-                out=w_codes[GATES[gate]][:, c, cols].bitcast(FP8X4),
-                scales=w_scales[GATES[gate]][:, c, cols],
+                out=w_codes[gate][:, c, cols].bitcast(FP8X4),
+                scales=w_scales[gate][:, c, cols],
                 in_=grouped[quarter][:].rearrange("p d t -> p (d t)"),
             )
 
         def where(m):
-            gate, g = divmod(m, GROUPS_PER_GATE)
+            index, chunk = divmod(m, CHUNKS)
+            gate, half = ORDER[index]
+            return gate, half, chunk, slice(chunk * CHUNK, (chunk + 1) * CHUNK), (half * CHUNKS + chunk) * PACK
+
+        def group_of(gate, g):
             half, chunk = divmod(g, CHUNKS)
-            return GATES[gate], half, chunk, slice(chunk * CHUNK, (chunk + 1) * CHUNK), g * PACK
+            return ORDER.index((gate, half)) * CHUNKS + chunk
 
         def plain_r(n, engine):
             g, t = divmod(n, PACK)
-            gate, half, chunk, tok, slot = where(g)
+            gate, half, chunk, tok, slot = where(group_of("r", g))
             ps = psum.tile([P, CHUNK], F32, name="xr" + str(n), tag="b")
             for x in range(X_PASSES):
                 nc.tensor.matmul(
@@ -220,7 +226,7 @@ def tile_lstmlayer_pa_kernel(tc, S, X, Uz, Ug, Ur, Uh, Wz, Wg, Wr, Wh, bz, bg, b
                     nc.sync.dma_start(out=out[rows, half * K_PASS : (half + 1) * K_PASS], in_=h[:])
 
         def multiply_sr(g):
-            gate, half, chunk, tok, slot = where(g)
+            gate, half, chunk, tok, slot = where(group_of("r", g))
             sr_tiles[g] = sr_pool.tile([P, CHUNK, PACK], BF16, name="sr" + str(g), tag="sr", align_bytes=64)
             nc.vector.tensor_tensor(
                 out=sr_tiles[g][:],
@@ -230,7 +236,7 @@ def tile_lstmlayer_pa_kernel(tc, S, X, Uz, Ug, Ur, Uh, Wz, Wg, Wr, Wh, bz, bg, b
             )
 
         def quantise_sr(g):
-            gate, half, chunk, tok, slot = where(g)
+            gate, half, chunk, tok, slot = where(group_of("r", g))
             nc.vector.quantize_mx(
                 out=sr_codes[:, half, tok].bitcast(FP8X4),
                 scales=sr_scales[:, half, tok],
@@ -238,7 +244,7 @@ def tile_lstmlayer_pa_kernel(tc, S, X, Uz, Ug, Ur, Uh, Wz, Wg, Wr, Wh, bz, bg, b
             )
 
         def multiply_zs(g):
-            gate, half, chunk, tok, slot = where(g)
+            gate, half, chunk, tok, slot = where(group_of("z", g))
             for i in range(ROWS):
                 place = zs[:, slot + i, :]
                 s_part = s_sb[:, chunk * ROWS + i, half * K_PASS : (half + 1) * K_PASS]
@@ -251,8 +257,8 @@ def tile_lstmlayer_pa_kernel(tc, S, X, Uz, Ug, Ur, Uh, Wz, Wg, Wr, Wh, bz, bg, b
         load_weight_half(0)
         nc.sync.dma_start(out=s_sb[:, ROWS:, :], in_=s_rows[:, ROWS:, :])
         load_weight_half(1)
-        load_weight_half(2)
         load_u("z")
+        load_weight_half(2)
         load_u("g")
 
         ident_bf16 = keep.tile([P, P], BF16)
@@ -314,46 +320,46 @@ def tile_lstmlayer_pa_kernel(tc, S, X, Uz, Ug, Ur, Uh, Wz, Wg, Wr, Wh, bz, bg, b
                 in_=sT[:, c, tok, :].rearrange("p m t -> p (m t)"),
             )
 
-        for n in range(0, 4):
+        for n in range(0, 8):
             plain_r(n, "scalar" if n % 2 == 0 else "vector")
         transpose_s(0, ("vector", "scalar"))
-        for n in range(4, 8):
-            plain_r(n, "scalar")
+        transpose_s(1, ("scalar", "scalar"))
         regroup_quarter(0, "vector")
         quantise_s(0, 0)
         regroup_quarter(1, "vector")
         quantise_s(0, 1)
         quantise_quarter(0)
         quantise_quarter(1)
-        for n in range(8, 12):
-            plain_r(n, "scalar")
-        transpose_s(1, ("scalar", "scalar"))
-        for n in range(12, 16):
-            plain_r(n, "scalar")
         bias_ps = psum.tile([P, P], BF16, name="bias_ps", tag="a")
         nc.tensor.transpose(bias_ps[:], bias_rows[:], ident_bf16[:])
         bias_col = keep.tile([P, (len(GATES) - 1) * D_TILES], F32)
         nc.scalar.copy(out=bias_col[:], in_=bias_ps[:, : (len(GATES) - 1) * D_TILES])
-        regroup_quarter(2, "scalar")
+        regroup_quarter(2, "vector")
         quantise_s(1, 0)
         quantise_s(1, 1)
 
         for m in range(N_GROUPS + 1):
-            if m < FIRST_Z:
-                mx_group_r(m)
-            elif m < N_GROUPS:
-                mx_group(m)
-            if m - 1 >= FIRST_Z:
-                sum_group(m - 1)
             if m + 2 < QUARTERS:
                 quantise_quarter(m + 2)
-            if m + 3 < QUARTERS:
-                regroup_quarter(m + 3, "scalar" if m == 0 else "vector")
+            if m + 3 < QUARTERS and m == 0:
+                regroup_quarter(m + 3, "scalar")
+            if m in SR_QUANTISED:
+                quantise_sr(SR_QUANTISED[m])
+            if m < N_GROUPS:
+                if where(m)[0] == "r":
+                    mx_group_r(m)
+                else:
+                    mx_group(m)
+            if m < 2:
+                for t in range(PACK):
+                    plain_r((2 + m) * PACK + t, "scalar")
+            if m >= 1 and where(m - 1)[0] != "r":
+                sum_group(m - 1)
+            if m + 3 < QUARTERS and m > 0:
+                regroup_quarter(m + 3, "vector")
             if m == 2:
                 load_u("h")
-            if 0 <= m - FIRST_Z - 2 < GROUPS_PER_GATE:
-                quantise_sr(m - FIRST_Z - 2)
-            if 0 <= m - FIRST_Z < GROUPS_PER_GATE:
-                multiply_sr(m - FIRST_Z)
-            if 0 <= m - FIRST_G < GROUPS_PER_GATE:
-                multiply_zs(m - FIRST_G)
+            if m in SR_FORMED:
+                multiply_sr(SR_FORMED[m])
+            if m in ZS_FORMED:
+                multiply_zs(ZS_FORMED[m])

@@ -56,6 +56,7 @@ def tile_lstmlayer_pa_kernel(tc, S, X, Uz, Ug, Ur, Uh, Wz, Wg, Wr, Wh, bz, bg, b
         h_pool = ctx.enter_context(tc.tile_pool(name="h", bufs=4))
         psum = ctx.enter_context(tc.psum_pool(name="psum", bufs=4, reuse_waits="tile"))
 
+        out_rows = out.rearrange("(p r) d -> p r d", p=P)
         x_sb = keep.tile([P, ROW_TILES, DIN], BF16)
         s_sb = keep.tile([P, ROW_TILES, D], BF16, align_bytes=64)
         xT = keep.tile([P, X_PASSES, TOKENS], BF16)
@@ -190,7 +191,8 @@ def tile_lstmlayer_pa_kernel(tc, S, X, Uz, Ug, Ur, Uh, Wz, Wg, Wr, Wh, bz, bg, b
         def sum_group(m):
             gate, half, chunk, tok, slot = where(m)
             sums = [psum.tile([P, K_PASS], F32, name="sum" + str(m) + "_" + str(i), tag="b") for i in range(ROWS)]
-            for i in range(ROWS):
+
+            def plain(i):
                 for x in range(X_PASSES):
                     nc.tensor.matmul(
                         out=sums[i][:],
@@ -199,8 +201,15 @@ def tile_lstmlayer_pa_kernel(tc, S, X, Uz, Ug, Ur, Uh, Wz, Wg, Wr, Wh, bz, bg, b
                         start=(x == 0),
                         stop=False,
                     )
+
+            together = m < N_GROUPS - 2
+            if together:
+                for i in range(ROWS):
+                    plain(i)
             for i in range(ROWS):
                 ps = sums[i]
+                if not together:
+                    plain(i)
                 for t in range(PACK):
                     nc.tensor.matmul(
                         out=ps[:, t * P : (t + 1) * P],
@@ -211,7 +220,6 @@ def tile_lstmlayer_pa_kernel(tc, S, X, Uz, Ug, Ur, Uh, Wz, Wg, Wr, Wh, bz, bg, b
                         stop=(t == PACK - 1),
                     )
                 r = chunk * ROWS + i
-                rows = slice(r * P, (r + 1) * P)
                 if gate == "z":
                     nc.scalar.activation(out=zs[:, slot + i, :], in_=ps[:], func=ACT.Tanh)
                 elif gate == "g":
@@ -223,7 +231,7 @@ def tile_lstmlayer_pa_kernel(tc, S, X, Uz, Ug, Ur, Uh, Wz, Wg, Wr, Wh, bz, bg, b
                         out=h[:], in0=rg[:, slot + i, :], scalar=1.0, in1=h[:], op0=ALU.add, op1=ALU.mult
                     )
                     nc.vector.tensor_tensor(out=h[:], in0=h[:], in1=zs[:, slot + i, :], op=ALU.add)
-                    nc.sync.dma_start(out=out[rows, half * K_PASS : (half + 1) * K_PASS], in_=h[:])
+                    nc.sync.dma_start(out=out_rows[:, r, half * K_PASS : (half + 1) * K_PASS], in_=h[:])
 
         def multiply_sr(g):
             gate, half, chunk, tok, slot = where(group_of("r", g))
@@ -250,8 +258,8 @@ def tile_lstmlayer_pa_kernel(tc, S, X, Uz, Ug, Ur, Uh, Wz, Wg, Wr, Wh, bz, bg, b
                 s_part = s_sb[:, chunk * ROWS + i, half * K_PASS : (half + 1) * K_PASS]
                 nc.vector.tensor_tensor(out=place, in0=place, in1=s_part, op=ALU.mult)
 
-        s_rows = S.rearrange("(r p) k -> p r k", p=P)
-        nc.sync.dma_start(out=x_sb[:], in_=X.rearrange("(r p) k -> p r k", p=P))
+        s_rows = S.rearrange("(p r) k -> p r k", p=P)
+        nc.sync.dma_start(out=x_sb[:], in_=X.rearrange("(p r) k -> p r k", p=P))
         load_u("r")
         nc.sync.dma_start(out=s_sb[:, :ROWS, :], in_=s_rows[:, :ROWS, :])
         load_weight_half(0)

@@ -27,13 +27,13 @@ D_TILES = D // P
 HALVES = D // K_PASS
 GATES = ("r", "z", "g", "h")
 GROUPS_PER_GATE = HALVES * CHUNKS
-ORDER = (("r", 0), ("z", 0), ("r", 1), ("z", 1), ("g", 0), ("g", 1), ("h", 0), ("h", 1))
+ORDER = (("r", 0), ("z", 0), ("r", 1), ("z", 1), ("g", 0), ("h", 0), ("g", 1), ("h", 1))
 N_GROUPS = len(ORDER) * CHUNKS
 QUARTERS = len(ORDER) * PASSES
 
 SR_FORMED = {3: 0, 4: 1, 6: 2, 7: 3}
 SR_QUANTISED = {5: 0, 6: 1, 8: 2, 9: 3}
-ZS_FORMED = {8: 0, 9: 1, 10: 2, 11: 3}
+ZS_FORMED = {8: 0, 9: 1, 13: 2, 14: 3}
 
 FLOPS = 2 * TOKENS * D * 4 * (D + DIN)
 
@@ -53,7 +53,7 @@ def tile_lstmlayer_pa_kernel(tc, S, X, Uz, Ug, Ur, Uh, Wz, Wg, Wr, Wh, bz, bg, b
         grouped_pool = ctx.enter_context(tc.tile_pool(name="grouped", bufs=2))
         sr_pool = ctx.enter_context(tc.tile_pool(name="sr", bufs=2))
         copied_pool = ctx.enter_context(tc.tile_pool(name="copied", bufs=8))
-        h_pool = ctx.enter_context(tc.tile_pool(name="h", bufs=4))
+        h_pool = ctx.enter_context(tc.tile_pool(name="h", bufs=8))
         psum = ctx.enter_context(tc.psum_pool(name="psum", bufs=4, reuse_waits="tile"))
 
         out_rows = out.rearrange("(p r) d -> p r d", p=P)
@@ -191,6 +191,12 @@ def tile_lstmlayer_pa_kernel(tc, S, X, Uz, Ug, Ur, Uh, Wz, Wg, Wr, Wh, bz, bg, b
         def sum_group(m):
             gate, half, chunk, tok, slot = where(m)
             sums = [psum.tile([P, K_PASS], F32, name="sum" + str(m) + "_" + str(i), tag="b") for i in range(ROWS)]
+            finished = []
+
+            def finish(i, h):
+                nc.vector.tensor_tensor(out=h[:], in0=h[:], in1=zs[:, slot + i, :], op=ALU.add)
+                r = chunk * ROWS + i
+                nc.sync.dma_start(out=out_rows[:, r, half * K_PASS : (half + 1) * K_PASS], in_=h[:])
 
             def plain(i):
                 for x in range(X_PASSES):
@@ -202,7 +208,7 @@ def tile_lstmlayer_pa_kernel(tc, S, X, Uz, Ug, Ur, Uh, Wz, Wg, Wr, Wh, bz, bg, b
                         stop=False,
                     )
 
-            together = m < N_GROUPS - 2
+            together = m < N_GROUPS - 3
             if together:
                 for i in range(ROWS):
                     plain(i)
@@ -219,7 +225,6 @@ def tile_lstmlayer_pa_kernel(tc, S, X, Uz, Ug, Ur, Uh, Wz, Wg, Wr, Wh, bz, bg, b
                         start=False,
                         stop=(t == PACK - 1),
                     )
-                r = chunk * ROWS + i
                 if gate == "z":
                     nc.scalar.activation(out=zs[:, slot + i, :], in_=ps[:], func=ACT.Tanh)
                 elif gate == "g":
@@ -230,8 +235,11 @@ def tile_lstmlayer_pa_kernel(tc, S, X, Uz, Ug, Ur, Uh, Wz, Wg, Wr, Wh, bz, bg, b
                     nc.vector.scalar_tensor_tensor(
                         out=h[:], in0=rg[:, slot + i, :], scalar=1.0, in1=h[:], op0=ALU.add, op1=ALU.mult
                     )
-                    nc.vector.tensor_tensor(out=h[:], in0=h[:], in1=zs[:, slot + i, :], op=ALU.add)
-                    nc.sync.dma_start(out=out_rows[:, r, half * K_PASS : (half + 1) * K_PASS], in_=h[:])
+                    finished.append((i, h))
+                    if i > 0:
+                        finish(*finished[i - 1])
+            if gate == "h":
+                finish(*finished[-1])
 
         def multiply_sr(g):
             gate, half, chunk, tok, slot = where(group_of("r", g))

@@ -208,14 +208,12 @@ def tile_lstmlayer_pa_kernel(tc, S, X, Uz, Ug, Ur, Uh, Wz, Wg, Wr, Wh, bz, bg, b
                         stop=False,
                     )
 
-            together = m < N_GROUPS - 3
-            if together:
-                for i in range(ROWS):
-                    plain(i)
+            run = ROWS // 2 if m >= N_GROUPS - 2 else ROWS
             for i in range(ROWS):
                 ps = sums[i]
-                if not together:
-                    plain(i)
+                if i % run == 0:
+                    for k in range(i, i + run):
+                        plain(k)
                 for t in range(PACK):
                     nc.tensor.matmul(
                         out=ps[:, t * P : (t + 1) * P],
@@ -267,10 +265,12 @@ def tile_lstmlayer_pa_kernel(tc, S, X, Uz, Ug, Ur, Uh, Wz, Wg, Wr, Wh, bz, bg, b
                 nc.vector.tensor_tensor(out=place, in0=place, in1=s_part, op=ALU.mult)
 
         s_rows = S.rearrange("(p r) k -> p r k", p=P)
-        nc.sync.dma_start(out=x_sb[:], in_=X.rearrange("(p r) k -> p r k", p=P))
+        x_rows = X.rearrange("(p r) k -> p r k", p=P)
+        nc.sync.dma_start(out=x_sb[:, :ROWS, :], in_=x_rows[:, :ROWS, :])
         load_u("r")
-        nc.sync.dma_start(out=s_sb[:, :ROWS, :], in_=s_rows[:, :ROWS, :])
+        nc.sync.dma_start(out=x_sb[:, ROWS:, :], in_=x_rows[:, ROWS:, :])
         load_weight_half(0)
+        nc.sync.dma_start(out=s_sb[:, :ROWS, :], in_=s_rows[:, :ROWS, :])
         nc.sync.dma_start(out=s_sb[:, ROWS:, :], in_=s_rows[:, ROWS:, :])
         load_weight_half(1)
         load_u("z")
@@ -296,7 +296,7 @@ def tile_lstmlayer_pa_kernel(tc, S, X, Uz, Ug, Ur, Uh, Wz, Wg, Wr, Wh, bz, bg, b
         nc.vector.memset(warm[:], 0.0)
         nc.scalar.activation(out=warm[:], in_=warm[:], func=ACT.Tanh)
 
-        for chunk in range(CHUNKS):
+        def transpose_x(chunk):
             for x in range(X_PASSES):
                 ps = psum.tile([P, ROWS, P], BF16, name="xt" + str(chunk) + str(x), tag="b")
                 for i in range(ROWS):
@@ -336,16 +336,22 @@ def tile_lstmlayer_pa_kernel(tc, S, X, Uz, Ug, Ur, Uh, Wz, Wg, Wr, Wh, bz, bg, b
                 in_=sT[:, c, tok, :].rearrange("p m t -> p (m t)"),
             )
 
-        for n in range(0, 8):
-            plain_r(n, "scalar" if n % 2 == 0 else "vector")
-        transpose_s(0, ("vector", "scalar"))
-        transpose_s(1, ("scalar", "scalar"))
+        transpose_x(0)
+        for n in range(0, 4):
+            plain_r(n, "vector" if n % 2 == 0 else "scalar")
+        transpose_x(1)
         regroup_quarter(0, "vector")
-        quantise_s(0, 0)
+        for n in range(4, 8):
+            plain_r(n, "scalar")
         regroup_quarter(1, "vector")
-        quantise_s(0, 1)
         quantise_quarter(0)
+        transpose_s(0, ("vector", "scalar"))
         quantise_quarter(1)
+        quantise_s(0, 0)
+        quantise_s(0, 1)
+        for n in range(8, 12):
+            plain_r(n, "scalar")
+        transpose_s(1, ("scalar", "scalar"))
         bias_ps = psum.tile([P, P], BF16, name="bias_ps", tag="a")
         nc.tensor.transpose(bias_ps[:], bias_rows[:], ident_bf16[:])
         bias_col = keep.tile([P, (len(GATES) - 1) * D_TILES], F32)
@@ -366,11 +372,9 @@ def tile_lstmlayer_pa_kernel(tc, S, X, Uz, Ug, Ur, Uh, Wz, Wg, Wr, Wh, bz, bg, b
                     mx_group_r(m)
                 else:
                     mx_group(m)
-            if m < 2:
-                for t in range(PACK):
-                    plain_r((2 + m) * PACK + t, "scalar")
-            if m >= 1 and where(m - 1)[0] != "r":
-                sum_group(m - 1)
+            if m == 1:
+                for n in range(12, 16):
+                    plain_r(n, "scalar")
             if m + 3 < QUARTERS and m > 0:
                 regroup_quarter(m + 3, "vector")
             if m == 2:
@@ -379,3 +383,5 @@ def tile_lstmlayer_pa_kernel(tc, S, X, Uz, Ug, Ur, Uh, Wz, Wg, Wr, Wh, bz, bg, b
                 multiply_sr(SR_FORMED[m])
             if m in ZS_FORMED:
                 multiply_zs(ZS_FORMED[m])
+            if m >= 1 and where(m - 1)[0] != "r":
+                sum_group(m - 1)

@@ -35,6 +35,8 @@ SR_FORMED = {3: 0, 4: 1, 6: 2, 7: 3}
 SR_QUANTISED = {5: 0, 6: 1, 8: 2, 9: 3}
 ZS_FORMED = {8: 0, 9: 1, 13: 2, 14: 3}
 
+WARM_UPS = 5
+
 FLOPS = 2 * TOKENS * D * 4 * (D + DIN)
 
 
@@ -175,8 +177,11 @@ def tile_lstmlayer_pa_kernel(tc, S, X, Uz, Ug, Ur, Uh, Wz, Wg, Wr, Wh, bz, bg, b
                 nc.vector.scalar_tensor_tensor(
                     out=place, in0=ps[:], scalar=br_col[:, half, t : t + 1], in1=place, op0=ALU.add, op1=ALU.add
                 )
-            for t in range(PACK):
-                nc.scalar.activation(out=rg[:, slot + t, :], in_=rg[:, slot + t, :], func=ACT.Tanh)
+
+        def tanh_r(m):
+            gate, half, chunk, tok, slot = where(m)
+            places = rg[:, slot : slot + PACK, :]
+            nc.scalar.activation(out=places, in_=places, func=ACT.Tanh)
 
         def mx_group(m):
             gate, half, chunk, tok, slot = where(m)
@@ -208,12 +213,17 @@ def tile_lstmlayer_pa_kernel(tc, S, X, Uz, Ug, Ur, Uh, Wz, Wg, Wr, Wh, bz, bg, b
                         stop=False,
                     )
 
-            run = ROWS // 2 if m >= N_GROUPS - 2 else ROWS
+            if m == N_GROUPS - 1:
+                runs = (2, 1, 1)
+            elif m == N_GROUPS - 2:
+                runs = (2, 2)
+            else:
+                runs = (ROWS,)
+            starts = {sum(runs[:k]): length for k, length in enumerate(runs)}
             for i in range(ROWS):
                 ps = sums[i]
-                if i % run == 0:
-                    for k in range(i, i + run):
-                        plain(k)
+                for k in range(i, i + starts.get(i, 0)):
+                    plain(k)
                 for t in range(PACK):
                     nc.tensor.matmul(
                         out=ps[:, t * P : (t + 1) * P],
@@ -259,10 +269,9 @@ def tile_lstmlayer_pa_kernel(tc, S, X, Uz, Ug, Ur, Uh, Wz, Wg, Wr, Wh, bz, bg, b
 
         def multiply_zs(g):
             gate, half, chunk, tok, slot = where(group_of("z", g))
-            for i in range(ROWS):
-                place = zs[:, slot + i, :]
-                s_part = s_sb[:, chunk * ROWS + i, half * K_PASS : (half + 1) * K_PASS]
-                nc.vector.tensor_tensor(out=place, in0=place, in1=s_part, op=ALU.mult)
+            places = zs[:, slot : slot + ROWS, :]
+            s_part = s_sb[:, chunk * ROWS : (chunk + 1) * ROWS, half * K_PASS : (half + 1) * K_PASS]
+            nc.vector.tensor_tensor(out=places, in0=places, in1=s_part, op=ALU.mult)
 
         s_rows = S.rearrange("(p r) k -> p r k", p=P)
         x_rows = X.rearrange("(p r) k -> p r k", p=P)
@@ -277,6 +286,8 @@ def tile_lstmlayer_pa_kernel(tc, S, X, Uz, Ug, Ur, Uh, Wz, Wg, Wr, Wh, bz, bg, b
         load_weight_half(2)
         load_u("g")
 
+        zeros = keep.tile([P, K_PASS], BF16)
+        nc.vector.memset(zeros[:], 0.0)
         ident_bf16 = keep.tile([P, P], BF16)
         make_identity(nc, ident_bf16[:])
         ident_f32 = keep.tile([P, P], F32)
@@ -336,6 +347,10 @@ def tile_lstmlayer_pa_kernel(tc, S, X, Uz, Ug, Ur, Uh, Wz, Wg, Wr, Wh, bz, bg, b
                 in_=sT[:, c, tok, :].rearrange("p m t -> p (m t)"),
             )
 
+        zero_ps = psum.tile([P, K_PASS], F32, name="zero_ps", tag="a")
+        for n in range(WARM_UPS):
+            nc.tensor.matmul(out=zero_ps[:], lhsT=zeros[:, :P], rhs=zeros[:], start=True, stop=True)
+
         transpose_x(0)
         for n in range(0, 4):
             plain_r(n, "vector" if n % 2 == 0 else "scalar")
@@ -349,8 +364,6 @@ def tile_lstmlayer_pa_kernel(tc, S, X, Uz, Ug, Ur, Uh, Wz, Wg, Wr, Wh, bz, bg, b
         quantise_quarter(1)
         quantise_s(0, 0)
         quantise_s(0, 1)
-        for n in range(8, 12):
-            plain_r(n, "scalar")
         transpose_s(1, ("scalar", "scalar"))
         bias_ps = psum.tile([P, P], BF16, name="bias_ps", tag="a")
         nc.tensor.transpose(bias_ps[:], bias_rows[:], ident_bf16[:])
@@ -367,14 +380,18 @@ def tile_lstmlayer_pa_kernel(tc, S, X, Uz, Ug, Ur, Uh, Wz, Wg, Wr, Wh, bz, bg, b
                 regroup_quarter(m + 3, "scalar")
             if m in SR_QUANTISED:
                 quantise_sr(SR_QUANTISED[m])
+            if m == N_GROUPS - 1:
+                sum_group(m - 1)
             if m < N_GROUPS:
                 if where(m)[0] == "r":
                     mx_group_r(m)
                 else:
                     mx_group(m)
-            if m == 1:
-                for n in range(12, 16):
-                    plain_r(n, "scalar")
+            if m in (1, 2):
+                for t in range(PACK):
+                    plain_r((m + 1) * PACK + t, "scalar")
+            if 1 <= m < N_GROUPS and where(m - 1)[0] == "r":
+                tanh_r(m - 1)
             if m + 3 < QUARTERS and m > 0:
                 regroup_quarter(m + 3, "vector")
             if m == 2:
@@ -383,5 +400,5 @@ def tile_lstmlayer_pa_kernel(tc, S, X, Uz, Ug, Ur, Uh, Wz, Wg, Wr, Wh, bz, bg, b
                 multiply_sr(SR_FORMED[m])
             if m in ZS_FORMED:
                 multiply_zs(ZS_FORMED[m])
-            if m >= 1 and where(m - 1)[0] != "r":
+            if m >= 1 and m != N_GROUPS - 1 and where(m - 1)[0] != "r":
                 sum_group(m - 1)

@@ -23,19 +23,30 @@ X_PASSES = DIN // P
 CHUNKS = TOKENS // CHUNK
 ROW_TILES = TOKENS // P
 ROWS = CHUNK // P
+ALL_TILES = range(PACK)
 D_TILES = D // P
 HALVES = D // K_PASS
 GATES = ("r", "z", "g", "h")
 GROUPS_PER_GATE = HALVES * CHUNKS
 ORDER = (("r", 0), ("z", 0), ("r", 1), ("z", 1), ("g", 0), ("h", 0), ("g", 1), ("h", 1))
-N_GROUPS = len(ORDER) * CHUNKS
+GROUPS = [(gate, half, chunk) for gate, half in ORDER[:-2] for chunk in range(CHUNKS)] + [
+    (gate, half, chunk) for chunk in range(CHUNKS) for gate, half in ORDER[-2:]
+]
+N_GROUPS = len(GROUPS)
 QUARTERS = len(ORDER) * PASSES
+
+REGROUPED = {1: (4,), 2: (5,), 3: (6, 7), 5: (9,), 6: (10,), 7: (11,), 8: (12,), 9: (13,), 10: (14,), 11: (15,)}
+SCALAR_REGROUPED = {4: (8,)}
+QUANTISED = {m: ((14, 15) if m == 12 else (m + 2,)) for m in range(13)}
 
 SR_FORMED = {3: 0, 4: 1, 6: 2, 7: 3}
 SR_QUANTISED = {5: 0, 6: 1, 8: 2, 9: 3}
-ZS_FORMED = {8: 0, 9: 1, 13: 2, 14: 3}
+ZS_FORMED = {10: 0, 11: 1, 12: 2, 13: 3}
 
-WARM_UPS = 5
+APART = (9, 12)
+SUMS_FIRST = (12,)
+
+WARM_UPS = 4
 
 FLOPS = 2 * TOKENS * D * 4 * (D + DIN)
 
@@ -52,10 +63,10 @@ def tile_lstmlayer_pa_kernel(tc, S, X, Uz, Ug, Ur, Uh, Wz, Wg, Wr, Wh, bz, bg, b
         u_pool = ctx.enter_context(tc.tile_pool(name="u", bufs=3))
         w_pool = ctx.enter_context(tc.tile_pool(name="w", bufs=2))
         raw_pool = ctx.enter_context(tc.tile_pool(name="raw", bufs=3))
-        grouped_pool = ctx.enter_context(tc.tile_pool(name="grouped", bufs=2))
+        grouped_pool = ctx.enter_context(tc.tile_pool(name="grouped", bufs=3))
         sr_pool = ctx.enter_context(tc.tile_pool(name="sr", bufs=2))
         copied_pool = ctx.enter_context(tc.tile_pool(name="copied", bufs=8))
-        h_pool = ctx.enter_context(tc.tile_pool(name="h", bufs=8))
+        h_pool = ctx.enter_context(tc.tile_pool(name="h", bufs=6))
         psum = ctx.enter_context(tc.psum_pool(name="psum", bufs=4, reuse_waits="tile"))
 
         out_rows = out.rearrange("(p r) d -> p r d", p=P)
@@ -71,6 +82,8 @@ def tile_lstmlayer_pa_kernel(tc, S, X, Uz, Ug, Ur, Uh, Wz, Wg, Wr, Wh, bz, bg, b
         zs = keep.tile([P, slots, CHUNK], F32)
         rg = keep.tile([P, slots, CHUNK], F32)
 
+        bg_wide = keep.tile([P, D], BF16)
+
         u_sb = {}
         raw = {}
         grouped = {}
@@ -78,6 +91,7 @@ def tile_lstmlayer_pa_kernel(tc, S, X, Uz, Ug, Ur, Uh, Wz, Wg, Wr, Wh, bz, bg, b
         w_scales = {}
         copied = {}
         sr_tiles = {}
+        h_tiles = {}
 
         def copy_on(engine, dest, source):
             if engine == "scalar":
@@ -130,13 +144,12 @@ def tile_lstmlayer_pa_kernel(tc, S, X, Uz, Ug, Ur, Uh, Wz, Wg, Wr, Wh, bz, bg, b
             )
 
         def where(m):
-            index, chunk = divmod(m, CHUNKS)
-            gate, half = ORDER[index]
+            gate, half, chunk = GROUPS[m]
             return gate, half, chunk, slice(chunk * CHUNK, (chunk + 1) * CHUNK), (half * CHUNKS + chunk) * PACK
 
         def group_of(gate, g):
             half, chunk = divmod(g, CHUNKS)
-            return ORDER.index((gate, half)) * CHUNKS + chunk
+            return GROUPS.index((gate, half, chunk))
 
         def plain_r(n, engine):
             g, t = divmod(n, PACK)
@@ -178,76 +191,116 @@ def tile_lstmlayer_pa_kernel(tc, S, X, Uz, Ug, Ur, Uh, Wz, Wg, Wr, Wh, bz, bg, b
                     out=place, in0=ps[:], scalar=br_col[:, half, t : t + 1], in1=place, op0=ALU.add, op1=ALU.add
                 )
 
-        def tanh_r(m):
+        def tanh_in_place(m):
             gate, half, chunk, tok, slot = where(m)
             places = rg[:, slot : slot + PACK, :]
-            nc.scalar.activation(out=places, in_=places, func=ACT.Tanh)
+            nc.scalar.activation(out=places, in_=places, func=ACT.Tanh, scale=(-1.0 if gate == "g" else 1.0))
 
-        def mx_group(m):
+        def mx_group(m, tiles):
             gate, half, chunk, tok, slot = where(m)
-            copied[m] = []
-            for t in range(PACK):
+            for t in tiles:
                 ps = mx_tile(m, t)
                 tile = copied_pool.tile([P, CHUNK], F32, name="copied" + str(m) + "_" + str(t), tag="copied")
                 column = (GATES.index(gate) - 1) * D_TILES + half * PACK + t
                 nc.scalar.activation(out=tile[:], in_=ps[:], func=ACT.Identity, bias=bias_col[:, column : column + 1])
-                copied[m].append(tile)
+                copied[m, t] = tile
 
-        def sum_group(m):
+        def in_place(m):
+            return where(m)[0] == "r" or m in APART
+
+        def apart_group(m):
             gate, half, chunk, tok, slot = where(m)
-            sums = [psum.tile([P, K_PASS], F32, name="sum" + str(m) + "_" + str(i), tag="b") for i in range(ROWS)]
-            finished = []
-
-            def finish(i, h):
-                nc.vector.tensor_tensor(out=h[:], in0=h[:], in1=zs[:, slot + i, :], op=ALU.add)
-                r = chunk * ROWS + i
-                nc.sync.dma_start(out=out_rows[:, r, half * K_PASS : (half + 1) * K_PASS], in_=h[:])
-
-            def plain(i):
+            cols = slice(half * K_PASS, (half + 1) * K_PASS)
+            for i in range(ROWS):
+                rows = slice((chunk * ROWS + i) * P, (chunk * ROWS + i + 1) * P)
+                ps = psum.tile([P, K_PASS], F32, name="xu" + str(m) + "_" + str(i), tag="b")
                 for x in range(X_PASSES):
                     nc.tensor.matmul(
-                        out=sums[i][:],
-                        lhsT=xT[:, x, (chunk * ROWS + i) * P : (chunk * ROWS + i + 1) * P],
-                        rhs=u_sb[gate][:, x, half * K_PASS : (half + 1) * K_PASS],
+                        out=ps[:],
+                        lhsT=xT[:, x, rows],
+                        rhs=u_sb[gate][:, x, cols],
                         start=(x == 0),
-                        stop=False,
+                        stop=(x == X_PASSES - 1),
                     )
-
-            if m == N_GROUPS - 1:
-                runs = (2, 1, 1)
-            elif m == N_GROUPS - 2:
-                runs = (2, 2)
-            else:
-                runs = (ROWS,)
-            starts = {sum(runs[:k]): length for k, length in enumerate(runs)}
+                nc.vector.tensor_tensor(out=rg[:, slot + i, :], in0=ps[:], in1=bg_wide[:, cols], op=ALU.add)
             for i in range(ROWS):
-                ps = sums[i]
-                for k in range(i, i + starts.get(i, 0)):
-                    plain(k)
-                for t in range(PACK):
-                    nc.tensor.matmul(
-                        out=ps[:, t * P : (t + 1) * P],
-                        lhsT=copied[m][t][:, i * P : (i + 1) * P],
-                        rhs=ident_f32[:],
-                        is_transpose=True,
-                        start=False,
-                        stop=(t == PACK - 1),
+                rows = slice((chunk * ROWS + i) * P, (chunk * ROWS + i + 1) * P)
+                ps = psum.tile([P, K_PASS], F32, name="sw" + str(m) + "_" + str(i), tag="a")
+                for c in range(PASSES):
+                    nc.tensor.matmul_mx(
+                        out=ps[:],
+                        lhsT=s_codes[:, c, rows].bitcast(FP8X4),
+                        lhsT_scale=s_scales[:, c, rows],
+                        rhs=w_codes[gate][:, c, cols].bitcast(FP8X4),
+                        rhs_scale=w_scales[gate][:, c, cols],
+                        start=(c == 0),
+                        stop=(c == PASSES - 1),
                     )
-                if gate == "z":
-                    nc.scalar.activation(out=zs[:, slot + i, :], in_=ps[:], func=ACT.Tanh)
-                elif gate == "g":
-                    nc.scalar.activation(out=rg[:, slot + i, :], in_=ps[:], func=ACT.Tanh, scale=-1.0)
-                else:
-                    h = h_pool.tile([P, K_PASS], F32, name="h" + str(m) + "_" + str(i), tag="h")
-                    nc.scalar.activation(out=h[:], in_=ps[:], func=ACT.Tanh)
-                    nc.vector.scalar_tensor_tensor(
-                        out=h[:], in0=rg[:, slot + i, :], scalar=1.0, in1=h[:], op0=ALU.add, op1=ALU.mult
-                    )
-                    finished.append((i, h))
-                    if i > 0:
-                        finish(*finished[i - 1])
-            if gate == "h":
-                finish(*finished[-1])
+                place = rg[:, slot + i, :]
+                nc.vector.tensor_tensor(out=place, in0=ps[:], in1=place, op=ALU.add)
+
+        def sum_group(m, tiles, runs):
+            gate, half, chunk, tok, slot = where(m)
+            width = len(tiles) * P
+            first = tiles[0] * P
+            part = slice(first, first + width)
+            cols = slice(half * K_PASS + first, half * K_PASS + first + width)
+            name = str(m) + "_" + str(tiles[0])
+            h_tiles[m, tiles] = []
+            for k, length in enumerate(runs):
+                run = range(sum(runs[:k]), sum(runs[:k]) + length)
+                sums = {}
+                for i in run:
+                    sums[i] = psum.tile([P, K_PASS], F32, name="sum" + name + str(i), tag="b")
+                    for x in range(X_PASSES):
+                        nc.tensor.matmul(
+                            out=sums[i][:, :width],
+                            lhsT=xT[:, x, (chunk * ROWS + i) * P : (chunk * ROWS + i + 1) * P],
+                            rhs=u_sb[gate][:, x, cols],
+                            start=(x == 0),
+                            stop=False,
+                        )
+                for i in run:
+                    ps = sums[i]
+                    for n, t in enumerate(tiles):
+                        nc.tensor.matmul(
+                            out=ps[:, n * P : (n + 1) * P],
+                            lhsT=copied[m, t][:, i * P : (i + 1) * P],
+                            rhs=ident_f32[:],
+                            is_transpose=True,
+                            start=False,
+                            stop=(n == len(tiles) - 1),
+                        )
+                    if gate == "z":
+                        dest = zs[:, slot + i, part]
+                    elif gate == "g":
+                        dest = rg[:, slot + i, part]
+                    else:
+                        h = h_pool.tile([P, K_PASS], F32, name="h" + name + str(i), tag="h")
+                        h_tiles[m, tiles].append(h)
+                        dest = h[:, :width]
+                    nc.scalar.activation(out=dest, in_=ps[:, :width], func=ACT.Tanh, scale=(-1.0 if gate == "g" else 1.0))
+
+        def combine(m, tiles):
+            gate, half, chunk, tok, slot = where(m)
+            first = tiles[0] * P
+            width = len(tiles) * P
+            part = slice(first, first + width)
+            cols = slice(half * K_PASS + first, half * K_PASS + first + width)
+
+            def finish(i):
+                place = zs[:, slot + i, part]
+                nc.vector.tensor_tensor(out=place, in0=h_tiles[m, tiles][i][:, :width], in1=place, op=ALU.add)
+                nc.sync.dma_start(out=out_rows[:, chunk * ROWS + i, cols], in_=place)
+
+            for i in range(ROWS):
+                h = h_tiles[m, tiles][i][:, :width]
+                nc.vector.scalar_tensor_tensor(
+                    out=h, in0=rg[:, slot + i, part], scalar=1.0, in1=h, op0=ALU.add, op1=ALU.mult
+                )
+                if i > 0:
+                    finish(i - 1)
+            finish(ROWS - 1)
 
         def multiply_sr(g):
             gate, half, chunk, tok, slot = where(group_of("r", g))
@@ -276,8 +329,8 @@ def tile_lstmlayer_pa_kernel(tc, S, X, Uz, Ug, Ur, Uh, Wz, Wg, Wr, Wh, bz, bg, b
         s_rows = S.rearrange("(p r) k -> p r k", p=P)
         x_rows = X.rearrange("(p r) k -> p r k", p=P)
         nc.sync.dma_start(out=x_sb[:, :ROWS, :], in_=x_rows[:, :ROWS, :])
-        load_u("r")
         nc.sync.dma_start(out=x_sb[:, ROWS:, :], in_=x_rows[:, ROWS:, :])
+        load_u("r")
         load_weight_half(0)
         nc.sync.dma_start(out=s_sb[:, :ROWS, :], in_=s_rows[:, :ROWS, :])
         nc.sync.dma_start(out=s_sb[:, ROWS:, :], in_=s_rows[:, ROWS:, :])
@@ -307,13 +360,13 @@ def tile_lstmlayer_pa_kernel(tc, S, X, Uz, Ug, Ur, Uh, Wz, Wg, Wr, Wh, bz, bg, b
         nc.vector.memset(warm[:], 0.0)
         nc.scalar.activation(out=warm[:], in_=warm[:], func=ACT.Tanh)
 
-        def transpose_x(chunk):
+        def transpose_x(chunk, engines):
             for x in range(X_PASSES):
                 ps = psum.tile([P, ROWS, P], BF16, name="xt" + str(chunk) + str(x), tag="b")
                 for i in range(ROWS):
                     nc.tensor.transpose(ps[:, i, :], x_sb[:, chunk * ROWS + i, x * P : (x + 1) * P], ident_bf16[:])
                 copy_on(
-                    "vector" if x == 0 else "scalar",
+                    engines[x],
                     xT[:, x, chunk * CHUNK : (chunk + 1) * CHUNK],
                     ps[:].rearrange("p i m -> p (i m)"),
                 )
@@ -351,10 +404,10 @@ def tile_lstmlayer_pa_kernel(tc, S, X, Uz, Ug, Ur, Uh, Wz, Wg, Wr, Wh, bz, bg, b
         for n in range(WARM_UPS):
             nc.tensor.matmul(out=zero_ps[:], lhsT=zeros[:, :P], rhs=zeros[:], start=True, stop=True)
 
-        transpose_x(0)
+        transpose_x(0, ("vector", "scalar"))
+        transpose_x(1, ("vector", "scalar"))
         for n in range(0, 4):
-            plain_r(n, "vector" if n % 2 == 0 else "scalar")
-        transpose_x(1)
+            plain_r(n, "scalar")
         regroup_quarter(0, "vector")
         for n in range(4, 8):
             plain_r(n, "scalar")
@@ -364,7 +417,10 @@ def tile_lstmlayer_pa_kernel(tc, S, X, Uz, Ug, Ur, Uh, Wz, Wg, Wr, Wh, bz, bg, b
         quantise_quarter(1)
         quantise_s(0, 0)
         quantise_s(0, 1)
+        plain_r(8, "scalar")
         transpose_s(1, ("scalar", "scalar"))
+        for n in range(9, 12):
+            plain_r(n, "scalar")
         bias_ps = psum.tile([P, P], BF16, name="bias_ps", tag="a")
         nc.tensor.transpose(bias_ps[:], bias_rows[:], ident_bf16[:])
         bias_col = keep.tile([P, (len(GATES) - 1) * D_TILES], F32)
@@ -372,33 +428,55 @@ def tile_lstmlayer_pa_kernel(tc, S, X, Uz, Ug, Ur, Uh, Wz, Wg, Wr, Wh, bz, bg, b
         regroup_quarter(2, "vector")
         quantise_s(1, 0)
         quantise_s(1, 1)
-
-        for m in range(N_GROUPS + 1):
-            if m + 2 < QUARTERS:
-                quantise_quarter(m + 2)
-            if m + 3 < QUARTERS and m == 0:
-                regroup_quarter(m + 3, "scalar")
+        for m in range(N_GROUPS - 1):
+            for quarter in QUANTISED.get(m, ()):
+                quantise_quarter(quarter)
+            if m == 0:
+                regroup_quarter(3, "scalar")
             if m in SR_QUANTISED:
                 quantise_sr(SR_QUANTISED[m])
-            if m == N_GROUPS - 1:
-                sum_group(m - 1)
-            if m < N_GROUPS:
-                if where(m)[0] == "r":
-                    mx_group_r(m)
-                else:
-                    mx_group(m)
-            if m in (1, 2):
-                for t in range(PACK):
-                    plain_r((m + 1) * PACK + t, "scalar")
-            if 1 <= m < N_GROUPS and where(m - 1)[0] == "r":
-                tanh_r(m - 1)
-            if m + 3 < QUARTERS and m > 0:
-                regroup_quarter(m + 3, "vector")
+            if m in SUMS_FIRST:
+                sum_group(m - 1, ALL_TILES, (ROWS,))
+            if where(m)[0] == "r":
+                mx_group_r(m)
+            elif m in APART:
+                apart_group(m)
+            else:
+                mx_group(m, ALL_TILES)
+            if m in SUMS_FIRST:
+                combine(m - 1, ALL_TILES)
+            if m == 2:
+                for n in range(12, 16):
+                    plain_r(n, "scalar")
+            if m >= 1 and in_place(m - 1):
+                tanh_in_place(m - 1)
+            for quarter in REGROUPED.get(m, ()):
+                regroup_quarter(quarter, "vector")
+            for quarter in SCALAR_REGROUPED.get(m, ()):
+                regroup_quarter(quarter, "scalar")
             if m == 2:
                 load_u("h")
+                nc.sync.dma_start(out=bg_wide[:], in_=bg.rearrange("o d -> (o d)").partition_broadcast(P))
             if m in SR_FORMED:
                 multiply_sr(SR_FORMED[m])
             if m in ZS_FORMED:
                 multiply_zs(ZS_FORMED[m])
-            if m >= 1 and m != N_GROUPS - 1 and where(m - 1)[0] != "r":
-                sum_group(m - 1)
+            summed = None
+            if m - 1 in APART:
+                if m - 1 not in SUMS_FIRST:
+                    summed = m - 2
+            elif m >= 1 and m not in APART and not in_place(m - 1):
+                summed = m - 1
+            if summed is not None:
+                sum_group(summed, ALL_TILES, (ROWS,))
+                if where(summed)[0] == "h":
+                    combine(summed, ALL_TILES)
+
+        last = N_GROUPS - 1
+        halves = (range(PACK // 2), range(PACK // 2, PACK))
+        mx_group(last, halves[0])
+        sum_group(last - 1, ALL_TILES, (ROWS,))
+        mx_group(last, halves[1])
+        for tiles in halves:
+            sum_group(last, tiles, (2, 2))
+            combine(last, tiles)

@@ -99,9 +99,14 @@ def tile_lstmlayer_pa_kernel(tc, S, X, Uz, Ug, Ur, Uh, Wz, Wg, Wr, Wh, bz, bg, b
             else:
                 nc.vector.tensor_copy(out=dest, in_=source)
 
-        def load_u(gate):
-            u_sb[gate] = u_pool.tile([P, X_PASSES, D], BF16, name="u_" + gate, tag="u")
-            nc.sync.dma_start(out=u_sb[gate][:], in_=u_dram[gate].rearrange("(x p) d -> p x d", p=P))
+        def load_u(gate, halves=range(HALVES)):
+            if gate not in u_sb:
+                u_sb[gate] = u_pool.tile([P, HALVES, X_PASSES, K_PASS], BF16, name="u_" + gate, tag="u")
+            for half in halves:
+                cols = slice(half * K_PASS, (half + 1) * K_PASS)
+                nc.sync.dma_start(
+                    out=u_sb[gate][:, half, :, :], in_=u_dram[gate][:, cols].rearrange("(x p) d -> p x d", p=P)
+                )
 
         def load_weight_half(index):
             gate, half = ORDER[index]
@@ -158,7 +163,7 @@ def tile_lstmlayer_pa_kernel(tc, S, X, Uz, Ug, Ur, Uh, Wz, Wg, Wr, Wh, bz, bg, b
             for x in range(X_PASSES):
                 nc.tensor.matmul(
                     out=ps[:],
-                    lhsT=u_sb["r"][:, x, half * K_PASS + t : (half + 1) * K_PASS : PACK],
+                    lhsT=u_sb["r"][:, half, x, t:K_PASS:PACK],
                     rhs=xT[:, x, tok],
                     start=(x == 0),
                     stop=(x == X_PASSES - 1),
@@ -218,7 +223,7 @@ def tile_lstmlayer_pa_kernel(tc, S, X, Uz, Ug, Ur, Uh, Wz, Wg, Wr, Wh, bz, bg, b
                     nc.tensor.matmul(
                         out=ps[:],
                         lhsT=xT[:, x, rows],
-                        rhs=u_sb[gate][:, x, cols],
+                        rhs=u_sb[gate][:, half, x, :],
                         start=(x == 0),
                         stop=(x == X_PASSES - 1),
                     )
@@ -244,7 +249,6 @@ def tile_lstmlayer_pa_kernel(tc, S, X, Uz, Ug, Ur, Uh, Wz, Wg, Wr, Wh, bz, bg, b
             width = len(tiles) * P
             first = tiles[0] * P
             part = slice(first, first + width)
-            cols = slice(half * K_PASS + first, half * K_PASS + first + width)
             name = str(m) + "_" + str(tiles[0])
             h_tiles[m, tiles] = []
             for k, length in enumerate(runs):
@@ -256,7 +260,7 @@ def tile_lstmlayer_pa_kernel(tc, S, X, Uz, Ug, Ur, Uh, Wz, Wg, Wr, Wh, bz, bg, b
                         nc.tensor.matmul(
                             out=sums[i][:, :width],
                             lhsT=xT[:, x, (chunk * ROWS + i) * P : (chunk * ROWS + i + 1) * P],
-                            rhs=u_sb[gate][:, x, cols],
+                            rhs=u_sb[gate][:, half, x, part],
                             start=(x == 0),
                             stop=False,
                         )
@@ -326,35 +330,36 @@ def tile_lstmlayer_pa_kernel(tc, S, X, Uz, Ug, Ur, Uh, Wz, Wg, Wr, Wh, bz, bg, b
             s_part = s_sb[:, chunk * ROWS : (chunk + 1) * ROWS, half * K_PASS : (half + 1) * K_PASS]
             nc.vector.tensor_tensor(out=places, in0=places, in1=s_part, op=ALU.mult)
 
+        zeros = keep.tile([P, K_PASS], BF16)
+        nc.vector.memset(zeros[:], 0.0)
+
         s_rows = S.rearrange("(p r) k -> p r k", p=P)
         x_rows = X.rearrange("(p r) k -> p r k", p=P)
         nc.sync.dma_start(out=x_sb[:, :ROWS, :], in_=x_rows[:, :ROWS, :])
         nc.sync.dma_start(out=x_sb[:, ROWS:, :], in_=x_rows[:, ROWS:, :])
-        load_u("r")
+        load_u("r", (0,))
         load_weight_half(0)
         nc.sync.dma_start(out=s_sb[:, :ROWS, :], in_=s_rows[:, :ROWS, :])
         nc.sync.dma_start(out=s_sb[:, ROWS:, :], in_=s_rows[:, ROWS:, :])
+        load_u("r", (1,))
+        bias_rows = keep.tile([P, P], BF16)
+        nc.vector.memset(bias_rows[:], 0.0)
+        for i, gate in enumerate(GATES[1:]):
+            nc.sync.dma_start(
+                out=bias_rows[i * D_TILES : (i + 1) * D_TILES, :],
+                in_=b_dram[gate].rearrange("o (j p) -> (o j) p", p=P),
+            )
+        br_col = keep.tile([P, HALVES, PACK], BF16)
+        nc.sync.dma_start(out=br_col[:], in_=br.rearrange("o (h p t) -> p (o h) t", p=P, t=PACK))
         load_weight_half(1)
         load_u("z")
         load_weight_half(2)
         load_u("g")
 
-        zeros = keep.tile([P, K_PASS], BF16)
-        nc.vector.memset(zeros[:], 0.0)
         ident_bf16 = keep.tile([P, P], BF16)
         make_identity(nc, ident_bf16[:])
         ident_f32 = keep.tile([P, P], F32)
         make_identity(nc, ident_f32[:])
-
-        bias_rows = keep.tile([P, P], BF16)
-        nc.vector.memset(bias_rows[:], 0.0)
-        for i, gate in enumerate(GATES[1:]):
-            nc.scalar.dma_start(
-                out=bias_rows[i * D_TILES : (i + 1) * D_TILES, :],
-                in_=b_dram[gate].rearrange("o (j p) -> (o j) p", p=P),
-            )
-        br_col = keep.tile([P, HALVES, PACK], BF16)
-        nc.scalar.dma_start(out=br_col[:], in_=br.rearrange("o (h p t) -> p (o h) t", p=P, t=PACK))
 
         warm = keep.tile([P, 1], F32)
         nc.vector.memset(warm[:], 0.0)
@@ -417,9 +422,8 @@ def tile_lstmlayer_pa_kernel(tc, S, X, Uz, Ug, Ur, Uh, Wz, Wg, Wr, Wh, bz, bg, b
         quantise_quarter(1)
         quantise_s(0, 0)
         quantise_s(0, 1)
-        plain_r(8, "scalar")
         transpose_s(1, ("scalar", "scalar"))
-        for n in range(9, 12):
+        for n in range(8, 12):
             plain_r(n, "scalar")
         bias_ps = psum.tile([P, P], BF16, name="bias_ps", tag="a")
         nc.tensor.transpose(bias_ps[:], bias_rows[:], ident_bf16[:])
@@ -456,6 +460,7 @@ def tile_lstmlayer_pa_kernel(tc, S, X, Uz, Ug, Ur, Uh, Wz, Wg, Wr, Wh, bz, bg, b
                 regroup_quarter(quarter, "scalar")
             if m == 2:
                 load_u("h")
+            if m == 8:
                 nc.sync.dma_start(out=bg_wide[:], in_=bg.rearrange("o d -> (o d)").partition_broadcast(P))
             if m in SR_FORMED:
                 multiply_sr(SR_FORMED[m])

@@ -35,8 +35,8 @@ GROUPS = [(gate, half, chunk) for gate, half in ORDER[:-2] for chunk in range(CH
 N_GROUPS = len(GROUPS)
 QUARTERS = len(ORDER) * PASSES
 
-REGROUPED = {1: (4,), 2: (5,), 3: (6, 7), 5: (9,), 6: (10,), 7: (11,), 8: (12,), 9: (13,), 10: (14,), 11: (15,)}
-SCALAR_REGROUPED = {4: (8,)}
+REGROUPED = {1: (4,), 2: (5,), 3: (6, 7), 6: (10,), 7: (11,), 9: (13,), 10: (14,), 11: (15,)}
+SCALAR_REGROUPED = {4: (8, 9), 9: (12,)}
 QUANTISED = {m: ((14, 15) if m == 12 else (m + 2,)) for m in range(13)}
 
 SR_FORMED = {3: 0, 4: 1, 6: 2, 7: 3}

from contextlib import ExitStack

import concourse.mybir as mybir
from concourse.masks import make_identity

F32 = mybir.dt.float32
BF16 = mybir.dt.bfloat16
U32 = mybir.dt.uint32
U8 = mybir.dt.uint8
FP8X4 = mybir.dt.float8_e4m3fn_x4
ACT = mybir.ActivationFunctionType
ALU = mybir.AluOpType

P = 128
PACK = 4
K_PASS = P * PACK
TOKENS = 1024
D = 1024
DIN = 256
CHUNK = 512
PASSES = D // K_PASS
X_PASSES = DIN // P
CHUNKS = TOKENS // CHUNK
ROW_TILES = TOKENS // P
ROWS = CHUNK // P
ALL_TILES = range(PACK)
D_TILES = D // P
HALVES = D // K_PASS
GATES = ("r", "z", "g", "h")
GROUPS_PER_GATE = HALVES * CHUNKS
ORDER = (("r", 0), ("z", 0), ("r", 1), ("z", 1), ("g", 0), ("h", 0), ("g", 1), ("h", 1))
GROUPS = [(gate, half, chunk) for gate, half in ORDER[:-2] for chunk in range(CHUNKS)] + [
    (gate, half, chunk) for chunk in range(CHUNKS) for gate, half in ORDER[-2:]
]
N_GROUPS = len(GROUPS)
QUARTERS = len(ORDER) * PASSES

REGROUPED = {1: (4,), 2: (5,), 3: (6, 7), 6: (10,), 7: (11,), 9: (13,), 10: (14,), 11: (15,)}
SCALAR_REGROUPED = {4: (8, 9), 9: (12,)}
QUANTISED = {m: ((14, 15) if m == 12 else (m + 2,)) for m in range(13)}

SR_FORMED = {3: 0, 4: 1, 6: 2, 7: 3}
SR_QUANTISED = {5: 0, 6: 1, 8: 2, 9: 3}
ZS_FORMED = {10: 0, 11: 1, 12: 2, 13: 3}

APART = (9, 12)
SUMS_FIRST = (12,)

WARM_UPS = 4

FLOPS = 2 * TOKENS * D * 4 * (D + DIN)


def tile_lstmlayer_pa_kernel(tc, S, X, Uz, Ug, Ur, Uh, Wz, Wg, Wr, Wh, bz, bg, br, bh, out):
    nc = tc.nc
    u_dram = {"r": Ur, "z": Uz, "g": Ug, "h": Uh}
    w_dram = {"r": Wr, "z": Wz, "g": Wg, "h": Wh}
    b_dram = {"z": bz, "g": bg, "h": bh}

    with ExitStack() as ctx:
        ctx.enter_context(tc.manual_schedule())
        keep = ctx.enter_context(tc.tile_pool(name="keep", bufs=1))
        u_pool = ctx.enter_context(tc.tile_pool(name="u", bufs=3))
        w_pool = ctx.enter_context(tc.tile_pool(name="w", bufs=2))
        raw_pool = ctx.enter_context(tc.tile_pool(name="raw", bufs=3))
        grouped_pool = ctx.enter_context(tc.tile_pool(name="grouped", bufs=3))
        sr_pool = ctx.enter_context(tc.tile_pool(name="sr", bufs=2))
        copied_pool = ctx.enter_context(tc.tile_pool(name="copied", bufs=8))
        h_pool = ctx.enter_context(tc.tile_pool(name="h", bufs=6))
        psum = ctx.enter_context(tc.psum_pool(name="psum", bufs=4, reuse_waits="tile"))

        out_rows = out.rearrange("(p r) d -> p r d", p=P)
        x_sb = keep.tile([P, ROW_TILES, DIN], BF16)
        s_sb = keep.tile([P, ROW_TILES, D], BF16, align_bytes=64)
        xT = keep.tile([P, X_PASSES, TOKENS], BF16)
        sT = keep.tile([P, PASSES, TOKENS, PACK], BF16, align_bytes=64)
        s_codes = keep.tile([P, PASSES, TOKENS], U32, align_bytes=64)
        s_scales = keep.tile([P, PASSES, TOKENS], U8, align_bytes=64)
        sr_codes = keep.tile([P, PASSES, TOKENS], U32, align_bytes=64)
        sr_scales = keep.tile([P, PASSES, TOKENS], U8, align_bytes=64)
        slots = GROUPS_PER_GATE * PACK
        zs = keep.tile([P, slots, CHUNK], F32)
        rg = keep.tile([P, slots, CHUNK], F32)

        bg_wide = keep.tile([P, D], BF16)

        u_sb = {}
        raw = {}
        grouped = {}
        w_codes = {}
        w_scales = {}
        copied = {}
        sr_tiles = {}
        h_tiles = {}

        def copy_on(engine, dest, source):
            if engine == "scalar":
                nc.scalar.copy(out=dest, in_=source)
            else:
                nc.vector.tensor_copy(out=dest, in_=source)

        def load_u(gate, halves=range(HALVES)):
            if gate not in u_sb:
                u_sb[gate] = u_pool.tile([P, HALVES, X_PASSES, K_PASS], BF16, name="u_" + gate, tag="u")
            for half in halves:
                cols = slice(half * K_PASS, (half + 1) * K_PASS)
                nc.sync.dma_start(
                    out=u_sb[gate][:, half, :, :], in_=u_dram[gate][:, cols].rearrange("(x p) d -> p x d", p=P)
                )

        def load_weight_half(index):
            gate, half = ORDER[index]
            cols = slice(half * K_PASS, (half + 1) * K_PASS)
            raw[index] = raw_pool.tile([P, PASSES, PACK, K_PASS], BF16, name="raw" + str(index), tag="raw")
            for c in range(PASSES):
                nc.sync.dma_start(
                    out=raw[index][:, c, :, :],
                    in_=w_dram[gate][c * K_PASS : (c + 1) * K_PASS, cols].rearrange("(p t) d -> p t d", t=PACK),
                )

        def regroup_quarter(quarter, engine):
            index, c = divmod(quarter, PASSES)
            gate = ORDER[index][0]
            grouped[quarter] = grouped_pool.tile(
                [P, K_PASS, PACK], BF16, name="grouped" + str(quarter), tag="grouped", align_bytes=64
            )
            source = raw[index][:, c, :, :]
            if gate == "r":
                dest = grouped[quarter][:].rearrange("p (i m) t -> p i m t", i=PACK)
                source = source.rearrange("p t (m i) -> p i m t", i=PACK)
            else:
                dest = grouped[quarter][:].rearrange("p (q i) t -> p q t i", i=4)
                source = source.rearrange("p t (q i) -> p q t i", i=4)
            copy_on(engine, dest, source)
            if c == PASSES - 1 and index + 3 < len(ORDER):
                load_weight_half(index + 3)

        def quantise_quarter(quarter):
            index, c = divmod(quarter, PASSES)
            gate, half = ORDER[index]
            cols = slice(half * K_PASS, (half + 1) * K_PASS)
            if gate not in w_codes:
                w_codes[gate] = w_pool.tile([P, PASSES, D], U32, name="w_codes_" + gate, tag="w_codes", align_bytes=64)
                w_scales[gate] = w_pool.tile([P, PASSES, D], U8, name="w_scales_" + gate, tag="w_scales", align_bytes=64)
            nc.vector.quantize_mx(
                out=w_codes[gate][:, c, cols].bitcast(FP8X4),
                scales=w_scales[gate][:, c, cols],
                in_=grouped[quarter][:].rearrange("p d t -> p (d t)"),
            )

        def where(m):
            gate, half, chunk = GROUPS[m]
            return gate, half, chunk, slice(chunk * CHUNK, (chunk + 1) * CHUNK), (half * CHUNKS + chunk) * PACK

        def group_of(gate, g):
            half, chunk = divmod(g, CHUNKS)
            return GROUPS.index((gate, half, chunk))

        def plain_r(n, engine):
            g, t = divmod(n, PACK)
            gate, half, chunk, tok, slot = where(group_of("r", g))
            ps = psum.tile([P, CHUNK], F32, name="xr" + str(n), tag="b")
            for x in range(X_PASSES):
                nc.tensor.matmul(
                    out=ps[:],
                    lhsT=u_sb["r"][:, half, x, t:K_PASS:PACK],
                    rhs=xT[:, x, tok],
                    start=(x == 0),
                    stop=(x == X_PASSES - 1),
                )
            copy_on(engine, rg[:, slot + t, :], ps[:])

        def mx_tile(m, t):
            gate, half, chunk, tok, slot = where(m)
            a_codes, a_scales = (sr_codes, sr_scales) if gate == "h" else (s_codes, s_scales)
            cols = slice(half * K_PASS + t * P, half * K_PASS + (t + 1) * P)
            ps = psum.tile([P, CHUNK], F32, name="mx" + str(m) + "_" + str(t), tag="a")
            for c in range(PASSES):
                nc.tensor.matmul_mx(
                    out=ps[:],
                    lhsT=w_codes[gate][:, c, cols].bitcast(FP8X4),
                    lhsT_scale=w_scales[gate][:, c, cols],
                    rhs=a_codes[:, c, tok].bitcast(FP8X4),
                    rhs_scale=a_scales[:, c, tok],
                    start=(c == 0),
                    stop=(c == PASSES - 1),
                )
            return ps

        def mx_group_r(m):
            gate, half, chunk, tok, slot = where(m)
            for t in range(PACK):
                ps = mx_tile(m, t)
                place = rg[:, slot + t, :]
                nc.vector.scalar_tensor_tensor(
                    out=place, in0=ps[:], scalar=br_col[:, half, t : t + 1], in1=place, op0=ALU.add, op1=ALU.add
                )

        def tanh_in_place(m):
            gate, half, chunk, tok, slot = where(m)
            places = rg[:, slot : slot + PACK, :]
            nc.scalar.activation(out=places, in_=places, func=ACT.Tanh, scale=(-1.0 if gate == "g" else 1.0))

        def mx_group(m, tiles):
            gate, half, chunk, tok, slot = where(m)
            for t in tiles:
                ps = mx_tile(m, t)
                tile = copied_pool.tile([P, CHUNK], F32, name="copied" + str(m) + "_" + str(t), tag="copied")
                column = (GATES.index(gate) - 1) * D_TILES + half * PACK + t
                nc.scalar.activation(out=tile[:], in_=ps[:], func=ACT.Identity, bias=bias_col[:, column : column + 1])
                copied[m, t] = tile

        def in_place(m):
            return where(m)[0] == "r" or m in APART

        def apart_group(m):
            gate, half, chunk, tok, slot = where(m)
            cols = slice(half * K_PASS, (half + 1) * K_PASS)
            for i in range(ROWS):
                rows = slice((chunk * ROWS + i) * P, (chunk * ROWS + i + 1) * P)
                ps = psum.tile([P, K_PASS], F32, name="xu" + str(m) + "_" + str(i), tag="b")
                for x in range(X_PASSES):
                    nc.tensor.matmul(
                        out=ps[:],
                        lhsT=xT[:, x, rows],
                        rhs=u_sb[gate][:, half, x, :],
                        start=(x == 0),
                        stop=(x == X_PASSES - 1),
                    )
                nc.vector.tensor_tensor(out=rg[:, slot + i, :], in0=ps[:], in1=bg_wide[:, cols], op=ALU.add)
            for i in range(ROWS):
                rows = slice((chunk * ROWS + i) * P, (chunk * ROWS + i + 1) * P)
                ps = psum.tile([P, K_PASS], F32, name="sw" + str(m) + "_" + str(i), tag="a")
                for c in range(PASSES):
                    nc.tensor.matmul_mx(
                        out=ps[:],
                        lhsT=s_codes[:, c, rows].bitcast(FP8X4),
                        lhsT_scale=s_scales[:, c, rows],
                        rhs=w_codes[gate][:, c, cols].bitcast(FP8X4),
                        rhs_scale=w_scales[gate][:, c, cols],
                        start=(c == 0),
                        stop=(c == PASSES - 1),
                    )
                place = rg[:, slot + i, :]
                nc.vector.tensor_tensor(out=place, in0=ps[:], in1=place, op=ALU.add)

        def sum_group(m, tiles, runs):
            gate, half, chunk, tok, slot = where(m)
            width = len(tiles) * P
            first = tiles[0] * P
            part = slice(first, first + width)
            name = str(m) + "_" + str(tiles[0])
            h_tiles[m, tiles] = []
            for k, length in enumerate(runs):
                run = range(sum(runs[:k]), sum(runs[:k]) + length)
                sums = {}
                for i in run:
                    sums[i] = psum.tile([P, K_PASS], F32, name="sum" + name + str(i), tag="b")
                    for x in range(X_PASSES):
                        nc.tensor.matmul(
                            out=sums[i][:, :width],
                            lhsT=xT[:, x, (chunk * ROWS + i) * P : (chunk * ROWS + i + 1) * P],
                            rhs=u_sb[gate][:, half, x, part],
                            start=(x == 0),
                            stop=False,
                        )
                for i in run:
                    ps = sums[i]
                    for n, t in enumerate(tiles):
                        nc.tensor.matmul(
                            out=ps[:, n * P : (n + 1) * P],
                            lhsT=copied[m, t][:, i * P : (i + 1) * P],
                            rhs=ident_f32[:],
                            is_transpose=True,
                            start=False,
                            stop=(n == len(tiles) - 1),
                        )
                    if gate == "z":
                        dest = zs[:, slot + i, part]
                    elif gate == "g":
                        dest = rg[:, slot + i, part]
                    else:
                        h = h_pool.tile([P, K_PASS], F32, name="h" + name + str(i), tag="h")
                        h_tiles[m, tiles].append(h)
                        dest = h[:, :width]
                    nc.scalar.activation(out=dest, in_=ps[:, :width], func=ACT.Tanh, scale=(-1.0 if gate == "g" else 1.0))

        def combine(m, tiles):
            gate, half, chunk, tok, slot = where(m)
            first = tiles[0] * P
            width = len(tiles) * P
            part = slice(first, first + width)
            cols = slice(half * K_PASS + first, half * K_PASS + first + width)

            def finish(i):
                place = zs[:, slot + i, part]
                nc.vector.tensor_tensor(out=place, in0=h_tiles[m, tiles][i][:, :width], in1=place, op=ALU.add)
                nc.sync.dma_start(out=out_rows[:, chunk * ROWS + i, cols], in_=place)

            for i in range(ROWS):
                h = h_tiles[m, tiles][i][:, :width]
                nc.vector.scalar_tensor_tensor(
                    out=h, in0=rg[:, slot + i, part], scalar=1.0, in1=h, op0=ALU.add, op1=ALU.mult
                )
                if i > 0:
                    finish(i - 1)
            finish(ROWS - 1)

        def multiply_sr(g):
            gate, half, chunk, tok, slot = where(group_of("r", g))
            sr_tiles[g] = sr_pool.tile([P, CHUNK, PACK], BF16, name="sr" + str(g), tag="sr", align_bytes=64)
            nc.vector.tensor_tensor(
                out=sr_tiles[g][:],
                in0=rg[:, slot : slot + PACK, :].rearrange("p t m -> p m t"),
                in1=sT[:, half, tok, :],
                op=ALU.mult,
            )

        def quantise_sr(g):
            gate, half, chunk, tok, slot = where(group_of("r", g))
            nc.vector.quantize_mx(
                out=sr_codes[:, half, tok].bitcast(FP8X4),
                scales=sr_scales[:, half, tok],
                in_=sr_tiles[g][:].rearrange("p m t -> p (m t)"),
            )

        def multiply_zs(g):
            gate, half, chunk, tok, slot = where(group_of("z", g))
            places = zs[:, slot : slot + ROWS, :]
            s_part = s_sb[:, chunk * ROWS : (chunk + 1) * ROWS, half * K_PASS : (half + 1) * K_PASS]
            nc.vector.tensor_tensor(out=places, in0=places, in1=s_part, op=ALU.mult)

        zeros = keep.tile([P, K_PASS], BF16)
        nc.vector.memset(zeros[:], 0.0)

        s_rows = S.rearrange("(p r) k -> p r k", p=P)
        x_rows = X.rearrange("(p r) k -> p r k", p=P)
        nc.sync.dma_start(out=x_sb[:, :ROWS, :], in_=x_rows[:, :ROWS, :])
        nc.sync.dma_start(out=x_sb[:, ROWS:, :], in_=x_rows[:, ROWS:, :])
        load_u("r", (0,))
        load_weight_half(0)
        nc.sync.dma_start(out=s_sb[:, :ROWS, :], in_=s_rows[:, :ROWS, :])
        nc.sync.dma_start(out=s_sb[:, ROWS:, :], in_=s_rows[:, ROWS:, :])
        load_u("r", (1,))
        bias_rows = keep.tile([P, P], BF16)
        nc.vector.memset(bias_rows[:], 0.0)
        for i, gate in enumerate(GATES[1:]):
            nc.sync.dma_start(
                out=bias_rows[i * D_TILES : (i + 1) * D_TILES, :],
                in_=b_dram[gate].rearrange("o (j p) -> (o j) p", p=P),
            )
        br_col = keep.tile([P, HALVES, PACK], BF16)
        nc.sync.dma_start(out=br_col[:], in_=br.rearrange("o (h p t) -> p (o h) t", p=P, t=PACK))
        load_weight_half(1)
        load_u("z")
        load_weight_half(2)
        load_u("g")

        ident_bf16 = keep.tile([P, P], BF16)
        make_identity(nc, ident_bf16[:])
        ident_f32 = keep.tile([P, P], F32)
        make_identity(nc, ident_f32[:])

        warm = keep.tile([P, 1], F32)
        nc.vector.memset(warm[:], 0.0)
        nc.scalar.activation(out=warm[:], in_=warm[:], func=ACT.Tanh)

        def transpose_x(chunk, engines):
            for x in range(X_PASSES):
                ps = psum.tile([P, ROWS, P], BF16, name="xt" + str(chunk) + str(x), tag="b")
                for i in range(ROWS):
                    nc.tensor.transpose(ps[:, i, :], x_sb[:, chunk * ROWS + i, x * P : (x + 1) * P], ident_bf16[:])
                copy_on(
                    engines[x],
                    xT[:, x, chunk * CHUNK : (chunk + 1) * CHUNK],
                    ps[:].rearrange("p i m -> p (i m)"),
                )

        s_words = s_sb[:].rearrange("p r k -> p (r k)").bitcast(F32)
        sT_words = sT[:].rearrange("p c m t -> p (c m t)").bitcast(F32)

        def transpose_s(chunk, engines):
            for c in range(PASSES):
                for pair in range(ROWS // 2):
                    r0 = chunk * ROWS + pair * 2
                    ps = psum.tile([P, 2, 2, P], F32, name="st" + str(r0) + str(c), tag="a")
                    for i in range(2):
                        start = (r0 + i) * (D // 2) + c * (K_PASS // 2)
                        for u in range(2):
                            nc.tensor.transpose(
                                ps[:, i, u, :], s_words[:, start + u : start + K_PASS // 2 : 2], ident_f32[:]
                            )
                    first = (c * TOKENS + r0 * P) * 2
                    copy_on(
                        engines[c],
                        sT_words[:, first : first + 4 * P].rearrange("p (i m u) -> p i m u", i=2, u=2),
                        ps[:].rearrange("p i u m -> p i m u"),
                    )

        def quantise_s(chunk, c):
            tok = slice(chunk * CHUNK, (chunk + 1) * CHUNK)
            nc.vector.quantize_mx(
                out=s_codes[:, c, tok].bitcast(FP8X4),
                scales=s_scales[:, c, tok],
                in_=sT[:, c, tok, :].rearrange("p m t -> p (m t)"),
            )

        zero_ps = psum.tile([P, K_PASS], F32, name="zero_ps", tag="a")
        for n in range(WARM_UPS):
            nc.tensor.matmul(out=zero_ps[:], lhsT=zeros[:, :P], rhs=zeros[:], start=True, stop=True)

        transpose_x(0, ("vector", "scalar"))
        transpose_x(1, ("vector", "scalar"))
        for n in range(0, 4):
            plain_r(n, "scalar")
        regroup_quarter(0, "vector")
        for n in range(4, 8):
            plain_r(n, "scalar")
        regroup_quarter(1, "vector")
        quantise_quarter(0)
        transpose_s(0, ("vector", "scalar"))
        quantise_quarter(1)
        quantise_s(0, 0)
        quantise_s(0, 1)
        transpose_s(1, ("scalar", "scalar"))
        for n in range(8, 12):
            plain_r(n, "scalar")
        bias_ps = psum.tile([P, P], BF16, name="bias_ps", tag="a")
        nc.tensor.transpose(bias_ps[:], bias_rows[:], ident_bf16[:])
        bias_col = keep.tile([P, (len(GATES) - 1) * D_TILES], F32)
        nc.scalar.copy(out=bias_col[:], in_=bias_ps[:, : (len(GATES) - 1) * D_TILES])
        regroup_quarter(2, "vector")
        quantise_s(1, 0)
        quantise_s(1, 1)
        for m in range(N_GROUPS - 1):
            for quarter in QUANTISED.get(m, ()):
                quantise_quarter(quarter)
            if m == 0:
                regroup_quarter(3, "scalar")
            if m in SR_QUANTISED:
                quantise_sr(SR_QUANTISED[m])
            if m in SUMS_FIRST:
                sum_group(m - 1, ALL_TILES, (ROWS,))
            if where(m)[0] == "r":
                mx_group_r(m)
            elif m in APART:
                apart_group(m)
            else:
                mx_group(m, ALL_TILES)
            if m in SUMS_FIRST:
                combine(m - 1, ALL_TILES)
            if m == 2:
                for n in range(12, 16):
                    plain_r(n, "scalar")
            if m >= 1 and in_place(m - 1):
                tanh_in_place(m - 1)
            for quarter in REGROUPED.get(m, ()):
                regroup_quarter(quarter, "vector")
            for quarter in SCALAR_REGROUPED.get(m, ()):
                regroup_quarter(quarter, "scalar")
            if m == 2:
                load_u("h")
            if m == 8:
                nc.sync.dma_start(out=bg_wide[:], in_=bg.rearrange("o d -> (o d)").partition_broadcast(P))
            if m in SR_FORMED:
                multiply_sr(SR_FORMED[m])
            if m in ZS_FORMED:
                multiply_zs(ZS_FORMED[m])
            summed = None
            if m - 1 in APART:
                if m - 1 not in SUMS_FIRST:
                    summed = m - 2
            elif m >= 1 and m not in APART and not in_place(m - 1):
                summed = m - 1
            if summed is not None:
                sum_group(summed, ALL_TILES, (ROWS,))
                if where(summed)[0] == "h":
                    combine(summed, ALL_TILES)

        last = N_GROUPS - 1
        halves = (range(PACK // 2), range(PACK // 2, PACK))
        mx_group(last, halves[0])
        sum_group(last - 1, ALL_TILES, (ROWS,))
        mx_group(last, halves[1])
        for tiles in halves:
            sum_group(last, tiles, (2, 2))
            combine(last, tiles)
